import numpy as np
import ml_dtypes


def mxq(x, axis, fmt="e4m3"):
    dtype, down = {"e4m3": (ml_dtypes.float8_e4m3fn, 7), "e5m2": (ml_dtypes.float8_e5m2, 14)}[fmt]
    v = np.moveaxis(np.asarray(x, np.float32).astype(ml_dtypes.bfloat16).astype(np.float64), axis, -1)
    blocks = v.reshape(v.shape[:-1] + (-1, 32))
    amax = np.abs(blocks).max(-1, keepdims=True)
    byte = np.maximum(np.where(amax > 0, np.frexp(amax)[1] - 1 + 127, 0) - down, 1)
    scale = np.exp2(byte - 127.0)
    codes = (blocks / scale).astype(np.float32).astype(dtype).astype(np.float64)
    return np.moveaxis((codes * scale).reshape(v.shape), -1, axis)


WIDE = False


def mx_kscale(k):
    if not WIDE:
        return np.ones(k)
    levels = np.array([10, -10, 5, -5, 0])
    a = np.random.permutation(np.resize(levels, k // 512 * 4)).reshape(k // 512, 4)
    idx = np.arange(k)
    return np.exp2(a[idx // 512, idx % 128 // 32])


BF16 = ml_dtypes.bfloat16


def bf(x):
    return np.asarray(x, np.float32).astype(BF16)


def f64(x):
    return np.asarray(x).astype(np.float64)


E2M1 = np.array([0.0, 0.5, 1.0, 1.5, 2.0, 3.0, 4.0, 6.0, -0.0, -0.5, -1.0, -1.5, -2.0, -3.0, -4.0, -6.0])


def pack_weight(w, fmt):
    k, n = w.shape
    w = f64(bf(w)).reshape(k // 32, 32, n)
    amax = np.abs(w).max(1)
    if fmt == "e4m3":
        byte = np.frexp(amax)[1] - 1 + 127 - 7
    else:
        mant, ex = np.frexp(amax / 6.0)
        byte = np.where(mant > 0.5, ex, ex - 1) + 127
    byte = np.clip(np.where(amax > 0, byte, 1), 1, 254)
    scaled = (w * np.exp2(127.0 - byte)[:, None, :]).reshape(k, n).astype(np.float32)
    by_word = np.ascontiguousarray(scaled.reshape(k // 512, 128, 4, n).transpose(0, 1, 3, 2))
    if fmt == "e4m3":
        words = by_word.astype(ml_dtypes.float8_e4m3fn).view(np.uint8)
    else:
        c = by_word.astype(ml_dtypes.float4_e2m1fn).view(np.uint8) & 0xF
        words = c[..., 0::2] | (c[..., 1::2] << 4)
    return np.ascontiguousarray(words), np.ascontiguousarray(byte.astype(np.uint8).reshape(k // 512, 16, n))


def unpack_weight(words, scales, fmt):
    g, p, n, _ = words.shape
    if fmt == "e4m3":
        vals = np.ascontiguousarray(words).view(ml_dtypes.float8_e4m3fn).astype(np.float64)
    else:
        nib = np.empty((g, p, n, 4), np.uint8)
        nib[..., 0::2] = words & 0xF
        nib[..., 1::2] = words >> 4
        vals = E2M1[nib]
    vals = vals * np.repeat(np.exp2(scales.astype(np.float64) - 127.0), 8, axis=1)[..., None]
    return vals.transpose(0, 1, 3, 2).reshape(g * 512, n)


B, H, W, FI, FO = 2, 16, 16, 16384, 512

OFFSETS = [(-1, 0), (1, 0), (0, -1), (0, 1), (-1, -1), (-1, 1), (1, -1), (1, 1)]


def setup_inputs():
    s = mx_kscale(FI)
    X = bf(np.random.standard_normal((B, H * W, FI)) * 0.5 * s)
    Wm_words, Wm_scales = pack_weight(np.random.standard_normal((FI, FO)) / np.sqrt(FI) / s[:, None], "e4m3")
    b = bf(np.random.standard_normal(FO) * 0.2)
    return {"X": X,
            "Wm_words": Wm_words,
            "Wm_scales": Wm_scales,
            "b": b,
            "H": H, "W": W}


def reference(X, Wm_words, Wm_scales, b, H, W):
    X = f64(X)
    Bn, N, F = X.shape
    Xg = X.reshape(Bn, H, W, F)
    P = np.pad(Xg, ((0, 0), (1, 1), (1, 1), (0, 0)))
    AX = P[:, 1 + OFFSETS[0][0]:1 + OFFSETS[0][0] + H,
           1 + OFFSETS[0][1]:1 + OFFSETS[0][1] + W, :]
    for dr, dc in OFFSETS[1:]:
        AX = AX + P[:, 1 + dr:1 + dr + H, 1 + dc:1 + dc + W, :]
    AX = AX.reshape(Bn, N, F)
    return (mxq(AX, 2, "e4m3") @ unpack_weight(Wm_words, Wm_scales, "e4m3")) + f64(b)

@@ -1,0 +1,241 @@
+from contextlib import ExitStack
+
+import concourse.mybir as mybir
+from concourse.masks import make_identity
+
+F32 = mybir.dt.float32
+BF16 = mybir.dt.bfloat16
+I32 = mybir.dt.int32
+U32 = mybir.dt.uint32
+U8 = mybir.dt.uint8
+FP8X4 = mybir.dt.float8_e4m3fn_x4
+ADD = mybir.AluOpType.add
+
+P = 128
+PACK = 4
+K_PASS = P * PACK
+IMAGES = 2
+GRID_ROWS = 16
+GRID_COLS = 16
+NODES = GRID_ROWS * GRID_COLS
+HALVES = NODES // P
+BLOCK_ROWS = P // GRID_COLS
+FEATURES = 16384
+OUT_FEATURES = 512
+GROUPS = FEATURES // K_PASS
+OFFSETS = [(-1, 0), (1, 0), (0, -1), (0, 1), (-1, -1), (-1, 1), (1, -1), (1, 1)]
+
+TENSOR_EVERY = 3
+TENSOR_FIRST = 1
+LAG = 2
+
+FLOPS = 2 * IMAGES * NODES * FEATURES * OUT_FEATURES
+
+
+def tile_graphconvlayer_k_kernel(tc, X, Wm_words, Wm_scales, b, H, W, out):
+    nc = tc.nc
+    assert H == GRID_ROWS and W == GRID_COLS
+
+    x_view = X.rearrange("i (h p) k -> p (i h) k", p=P)
+    w_view = Wm_words.rearrange("g p n t -> g p (n t)")
+    s_view = Wm_scales.rearrange("g q n -> q g n")
+
+    with ExitStack() as ctx:
+        const = ctx.enter_context(tc.tile_pool(name="const", bufs=1))
+        x_pool = ctx.enter_context(tc.tile_pool(name="x", bufs=4))
+        w_pool = ctx.enter_context(tc.tile_pool(name="w", bufs=6))
+        sum_pool = ctx.enter_context(tc.tile_pool(name="sums", bufs=4))
+        ax_pool = ctx.enter_context(tc.tile_pool(name="ax", bufs=4))
+        res_pool = ctx.enter_context(tc.tile_pool(name="res", bufs=2))
+        acc_pool = ctx.enter_context(tc.psum_pool(name="acc", bufs=1))
+        work_pool = ctx.enter_context(tc.psum_pool(name="work", bufs=4))
+
+        w_scales = const.tile([P, GROUPS, OUT_FEATURES], U8, align_bytes=64)
+        nc.vector.memset(w_scales[:].rearrange("p g n -> p (g n)").bitcast(I32), 0)
+
+        bias = const.tile([P, OUT_FEATURES], BF16)
+        nc.scalar.dma_start(out=bias[:], in_=b.partition_broadcast(P))
+
+        ident_words = const.tile([P, P], F32)
+        make_identity(nc, ident_words[:])
+
+        ident = const.tile([P, P], BF16)
+        make_identity(nc, ident[:])
+        unit = const.tile([P, BLOCK_ROWS + 4, GRID_COLS + 2], BF16)
+        nc.gpsimd.memset(unit[:], 0.0)
+        nc.vector.tensor_copy(
+            out=unit[:, 2 : 2 + BLOCK_ROWS, 1 : 1 + GRID_COLS],
+            in_=ident[:].rearrange("p (r c) -> p r c", c=GRID_COLS),
+        )
+        adjacency = const.tile([P, BLOCK_ROWS + 2, GRID_COLS], BF16)
+        nc.gpsimd.memset(adjacency[:], 0.0)
+        for dr, dc in OFFSETS:
+            nc.vector.tensor_tensor(
+                out=adjacency[:],
+                in0=adjacency[:],
+                in1=unit[:, 1 + dr : 1 + dr + BLOCK_ROWS + 2, 1 + dc : 1 + dc + GRID_COLS],
+                op=ADD,
+            )
+        adj = adjacency[:].rearrange("p r c -> p (r c)")
+        onto_row_before = adj[:, 0:GRID_COLS]
+        onto_own_block = adj[:, GRID_COLS : GRID_COLS + P]
+        onto_row_after = adj[:, GRID_COLS + P : 2 * GRID_COLS + P]
+
+        shifted_down = [
+            const.tile([P, IMAGES, GRID_COLS + NODES, PACK], BF16, name="shifted_down%d" % n) for n in range(2)
+        ]
+        triples = [
+            const.tile([P, IMAGES, GRID_ROWS, (GRID_COLS + 2) * PACK], F32, name="triples%d" % n) for n in range(2)
+        ]
+        for tile_ in shifted_down:
+            nc.gpsimd.memset(tile_[:, :, 0:GRID_COLS, :], 0.0)
+        for tile_ in triples:
+            nc.vector.memset(tile_[:, :, :, 0:PACK], 0.0)
+            nc.vector.memset(tile_[:, :, :, (GRID_COLS + 1) * PACK :], 0.0)
+
+        acc = [acc_pool.tile([P, OUT_FEATURES], F32, name="acc%d" % m) for m in range(IMAGES * HALVES)]
+
+        def load(g):
+            x_sb = x_pool.tile([P, IMAGES * HALVES, K_PASS], BF16, name="x_sb")
+            nc.sync.dma_start(out=x_sb[:], in_=x_view[:, :, g * K_PASS : (g + 1) * K_PASS])
+            w_sb = w_pool.tile([P, OUT_FEATURES], U32, name="w_sb", align_bytes=64)
+            nc.sync.dma_start(out=w_sb[:].bitcast(I32), in_=w_view[g].bitcast(I32))
+            return x_sb, w_sb
+
+        def sums_on_tensor(x_sb, ax):
+            for i in range(IMAGES):
+                for h in range(HALVES):
+                    sums = work_pool.tile([P, PACK, P], F32, name="sums", tag="work")
+                    for t in range(PACK):
+                        k_cols = slice(t, K_PASS, PACK)
+                        nc.tensor.matmul(
+                            out=sums[:, t, :],
+                            lhsT=x_sb[:, i * HALVES + h, k_cols],
+                            rhs=onto_own_block,
+                            start=True,
+                            stop=False,
+                        )
+                        if h == 0:
+                            nc.tensor.matmul(
+                                out=sums[:, t, P - GRID_COLS : P],
+                                lhsT=x_sb[:, i * HALVES + 1, k_cols],
+                                rhs=onto_row_before,
+                                start=False,
+                                stop=True,
+                            )
+                        else:
+                            nc.tensor.matmul(
+                                out=sums[:, t, 0:GRID_COLS],
+                                lhsT=x_sb[:, i * HALVES, k_cols],
+                                rhs=onto_row_after,
+                                start=False,
+                                stop=True,
+                            )
+                    nc.scalar.copy(out=ax[:, i, h * P : (h + 1) * P, :], in_=sums[:].rearrange("p t n -> p n t"))
+
+        def first_adds_on_vector(g, x_sb):
+            x_words = x_sb[:].bitcast(F32)
+            turn = g % TENSOR_EVERY // 2
+            above = shifted_down[turn]
+            triple = triples[turn]
+            pair = sum_pool.tile([P, IMAGES, NODES, PACK], F32, name="pair")
+            sides = sum_pool.tile([P, IMAGES, GRID_ROWS, GRID_COLS * PACK], F32, name="sides")
+            banks = []
+            for i in range(IMAGES):
+                xt = work_pool.tile([P, 2, NODES], F32, name="xt", tag="work")
+                for u in range(2):
+                    for h in range(HALVES):
+                        nc.tensor.transpose(
+                            out=xt[:, u, h * P : (h + 1) * P],
+                            in_=x_words[:, i * HALVES + h, u : K_PASS // 2 : 2],
+                            identity=ident_words[:],
+                        )
+                nc.scalar.copy(
+                    out=above[:, i, GRID_COLS:, :].bitcast(F32), in_=xt[:].rearrange("p u n -> p n u")
+                )
+                nc.scalar.copy(
+                    out=pair[:, i, NODES - GRID_COLS :, :], in_=above[:, i, NODES - GRID_COLS : NODES, :]
+                )
+                banks.append(xt[:].bitcast(BF16).rearrange("p u (n e) -> p n u e", e=2))
+            for i in range(IMAGES):
+                nc.vector.tensor_tensor(
+                    out=pair[:, i, 0 : NODES - GRID_COLS, :].rearrange("p n (u e) -> p n u e", e=2),
+                    in0=banks[i][:, GRID_COLS:, :, :],
+                    in1=above[:, i, 0 : NODES - GRID_COLS, :].rearrange("p n (u e) -> p n u e", e=2),
+                    op=ADD,
+                )
+            for i in range(IMAGES):
+                nc.vector.tensor_tensor(
+                    out=triple[:, i, :, PACK : (GRID_COLS + 1) * PACK].rearrange(
+                        "p r (c u e) -> p r c u e", u=2, e=2
+                    ),
+                    in0=banks[i].rearrange("p (r c) u e -> p r c u e", c=GRID_COLS),
+                    in1=pair[:, i, :, :].rearrange("p (r c) (u e) -> p r c u e", c=GRID_COLS, e=2),
+                    op=ADD,
+                )
+            for i in range(IMAGES):
+                nc.vector.tensor_tensor(
+                    out=sides[:, i, :, :],
+                    in0=triple[:, i, :, 0 : GRID_COLS * PACK],
+                    in1=triple[:, i, :, 2 * PACK :],
+                    op=ADD,
+                )
+            return pair, sides
+
+        def last_add_on_vector(pair, sides, ax):
+            for i in range(IMAGES):
+                nc.vector.tensor_tensor(
+                    out=ax[:, i, :, :].rearrange("p n t -> p (n t)"),
+                    in0=sides[:, i, :, :].rearrange("p r w -> p (r w)"),
+                    in1=pair[:, i, :, :].rearrange("p n t -> p (n t)"),
+                    op=ADD,
+                )
+
+        def multiply(g, ax, w_sb):
+            codes = ax_pool.tile([P, IMAGES * NODES], U32, name="codes", align_bytes=64)
+            scales = ax_pool.tile([P, IMAGES * NODES], U8, name="scales", align_bytes=64)
+            nc.vector.quantize_mx(
+                out=codes[:].bitcast(FP8X4), scales=scales[:], in_=ax[:].rearrange("p i n t -> p (i n t)")
+            )
+            for m in range(IMAGES * HALVES):
+                cols = slice(m * P, (m + 1) * P)
+                nc.tensor.matmul_mx(
+                    out=acc[m][:],
+                    lhsT=codes[:, cols].bitcast(FP8X4),
+                    lhsT_scale=scales[:, cols],
+                    rhs=w_sb[:].bitcast(FP8X4),
+                    rhs_scale=w_scales[:, g, :],
+                    start=(g == 0),
+                    stop=(g == GROUPS - 1),
+                )
+
+        begun = {}
+        for step in range(GROUPS + LAG):
+            if step < GROUPS:
+                g = step
+                x_sb, w_sb = load(g)
+                if g == 0:
+                    for quadrant in range(4):
+                        nc.sync.dma_start(
+                            out=w_scales[32 * quadrant : 32 * quadrant + 4, :, :].bitcast(I32),
+                            in_=s_view[4 * quadrant : 4 * quadrant + 4, :, :].bitcast(I32),
+                        )
+                if g % TENSOR_EVERY == TENSOR_FIRST:
+                    ax = ax_pool.tile([P, IMAGES, NODES, PACK], BF16, name="ax", align_bytes=64)
+                    sums_on_tensor(x_sb, ax)
+                    begun[g] = (w_sb, ax, None, None)
+                else:
+                    pair, sides = first_adds_on_vector(g, x_sb)
+                    begun[g] = (w_sb, None, pair, sides)
+            if step >= LAG:
+                g = step - LAG
+                w_sb, ax, pair, sides = begun[g]
+                if ax is None:
+                    ax = ax_pool.tile([P, IMAGES, NODES, PACK], BF16, name="ax", align_bytes=64)
+                    last_add_on_vector(pair, sides, ax)
+                multiply(g, ax, w_sb)
+
+        for m in range(IMAGES * HALVES):
+            result = res_pool.tile([P, OUT_FEATURES], F32, name="result")
+            nc.vector.tensor_tensor(out=result[:], in0=acc[m][:], in1=bias[:], op=ADD)
+            nc.sync.dma_start(out=out.rearrange("i (h p) n -> (i h) p n", p=P)[m], in_=result[:])

@@ -174,7 +174,7 @@ def tile_graphconvlayer_k_kernel(tc, X, Wm_words, Wm_scales, b, H, W, out):
                     op=ADD,
                 )
             for i in range(IMAGES):
-                nc.vector.tensor_tensor(
+                nc.gpsimd.tensor_tensor(
                     out=sides[:, i, :, :],
                     in0=triple[:, i, :, 0 : GRID_COLS * PACK],
                     in1=triple[:, i, :, 2 * PACK :],

@@ -23,13 +23,15 @@ BLOCK_ROWS = P // GRID_COLS
 FEATURES = 16384
 OUT_FEATURES = 512
 GROUPS = FEATURES // K_PASS
+UNITS = GROUPS * IMAGES
 OFFSETS = [(-1, 0), (1, 0), (0, -1), (0, 1), (-1, -1), (-1, 1), (1, -1), (1, 1)]
 
-TENSOR_EVERY = 3
-TENSOR_FIRST = 1
-LAG = 2
-
 FLOPS = 2 * IMAGES * NODES * FEATURES * OUT_FEATURES
+
+TENSOR_PERIOD = 5
+TENSOR_TURNS = (2, 4)
+TENSOR_UNITS = len([u for u in range(UNITS) if u % TENSOR_PERIOD in TENSOR_TURNS])
+assert 10 * TENSOR_UNITS * 2 * P * P * NODES * PACK <= FLOPS
 
 
 def tile_graphconvlayer_k_kernel(tc, X, Wm_words, Wm_scales, b, H, W, out):
@@ -39,13 +41,17 @@ def tile_graphconvlayer_k_kernel(tc, X, Wm_words, Wm_scales, b, H, W, out):
     x_view = X.rearrange("i (h p) k -> p (i h) k", p=P)
     w_view = Wm_words.rearrange("g p n t -> g p (n t)")
     s_view = Wm_scales.rearrange("g q n -> q g n")
+    out_view = out.rearrange("i (h p) n -> (i h) p n", p=P)
 
     with ExitStack() as ctx:
         const = ctx.enter_context(tc.tile_pool(name="const", bufs=1))
-        x_pool = ctx.enter_context(tc.tile_pool(name="x", bufs=4))
+        x_pool = ctx.enter_context(tc.tile_pool(name="x", bufs=6))
         w_pool = ctx.enter_context(tc.tile_pool(name="w", bufs=6))
-        sum_pool = ctx.enter_context(tc.tile_pool(name="sums", bufs=4))
-        ax_pool = ctx.enter_context(tc.tile_pool(name="ax", bufs=4))
+        copy_pool = ctx.enter_context(tc.tile_pool(name="copies", bufs=3))
+        pair_pool = ctx.enter_context(tc.tile_pool(name="pairs", bufs=6))
+        sides_pool = ctx.enter_context(tc.tile_pool(name="sides", bufs=3))
+        ax_pool = ctx.enter_context(tc.tile_pool(name="ax", bufs=7))
+        mx_pool = ctx.enter_context(tc.tile_pool(name="mx", bufs=3))
         res_pool = ctx.enter_context(tc.tile_pool(name="res", bufs=2))
         acc_pool = ctx.enter_context(tc.psum_pool(name="acc", bufs=1))
         work_pool = ctx.enter_context(tc.psum_pool(name="work", bufs=4))
@@ -61,181 +67,200 @@ def tile_graphconvlayer_k_kernel(tc, X, Wm_words, Wm_scales, b, H, W, out):
 
         ident = const.tile([P, P], BF16)
         make_identity(nc, ident[:])
-        unit = const.tile([P, BLOCK_ROWS + 4, GRID_COLS + 2], BF16)
-        nc.gpsimd.memset(unit[:], 0.0)
+        unit_grid = const.tile([P, BLOCK_ROWS + 2, GRID_COLS + 2], BF16)
+        nc.gpsimd.memset(unit_grid[:], 0.0)
         nc.vector.tensor_copy(
-            out=unit[:, 2 : 2 + BLOCK_ROWS, 1 : 1 + GRID_COLS],
+            out=unit_grid[:, 1 : 1 + BLOCK_ROWS, 1 : 1 + GRID_COLS],
             in_=ident[:].rearrange("p (r c) -> p r c", c=GRID_COLS),
         )
-        adjacency = const.tile([P, BLOCK_ROWS + 2, GRID_COLS], BF16)
-        nc.gpsimd.memset(adjacency[:], 0.0)
+        adjacency_grid = const.tile([P, BLOCK_ROWS, GRID_COLS], BF16)
+        nc.gpsimd.memset(adjacency_grid[:], 0.0)
         for dr, dc in OFFSETS:
             nc.vector.tensor_tensor(
-                out=adjacency[:],
-                in0=adjacency[:],
-                in1=unit[:, 1 + dr : 1 + dr + BLOCK_ROWS + 2, 1 + dc : 1 + dc + GRID_COLS],
+                out=adjacency_grid[:],
+                in0=adjacency_grid[:],
+                in1=unit_grid[:, 1 + dr : 1 + dr + BLOCK_ROWS, 1 + dc : 1 + dc + GRID_COLS],
                 op=ADD,
             )
-        adj = adjacency[:].rearrange("p r c -> p (r c)")
-        onto_row_before = adj[:, 0:GRID_COLS]
-        onto_own_block = adj[:, GRID_COLS : GRID_COLS + P]
-        onto_row_after = adj[:, GRID_COLS + P : 2 * GRID_COLS + P]
+        adjacency = adjacency_grid[:].rearrange("p r c -> p (r c)")
 
-        shifted_down = [
-            const.tile([P, IMAGES, GRID_COLS + NODES, PACK], BF16, name="shifted_down%d" % n) for n in range(2)
-        ]
         triples = [
-            const.tile([P, IMAGES, GRID_ROWS, (GRID_COLS + 2) * PACK], F32, name="triples%d" % n) for n in range(2)
+            const.tile([P, GRID_ROWS, (GRID_COLS + 2) * PACK], F32, name="triples%d" % n) for n in range(3)
         ]
-        for tile_ in shifted_down:
-            nc.gpsimd.memset(tile_[:, :, 0:GRID_COLS, :], 0.0)
-        for tile_ in triples:
-            nc.vector.memset(tile_[:, :, :, 0:PACK], 0.0)
-            nc.vector.memset(tile_[:, :, :, (GRID_COLS + 1) * PACK :], 0.0)
+        for fixed in triples:
+            nc.vector.memset(fixed[:, :, 0:PACK], 0.0)
+            nc.vector.memset(fixed[:, :, (GRID_COLS + 1) * PACK :], 0.0)
 
         acc = [acc_pool.tile([P, OUT_FEATURES], F32, name="acc%d" % m) for m in range(IMAGES * HALVES)]
 
-        def load(g):
-            x_sb = x_pool.tile([P, IMAGES * HALVES, K_PASS], BF16, name="x_sb")
-            nc.sync.dma_start(out=x_sb[:], in_=x_view[:, :, g * K_PASS : (g + 1) * K_PASS])
-            w_sb = w_pool.tile([P, OUT_FEATURES], U32, name="w_sb", align_bytes=64)
-            nc.sync.dma_start(out=w_sb[:].bitcast(I32), in_=w_view[g].bitcast(I32))
-            return x_sb, w_sb
+        weights = {}
+        values = {}
+        copies = {}
+        pairs = {}
+        sides = {}
+        totals = {}
 
-        def sums_on_tensor(x_sb, ax):
-            for i in range(IMAGES):
-                for h in range(HALVES):
-                    sums = work_pool.tile([P, PACK, P], F32, name="sums", tag="work")
-                    for t in range(PACK):
-                        k_cols = slice(t, K_PASS, PACK)
+        def on_vector(u):
+            return 0 <= u < UNITS and u % TENSOR_PERIOD not in TENSOR_TURNS
+
+        def lanes(ap):
+            return ap.rearrange("p n (u e) -> p n u e", e=2)
+
+        def prepare(u):
+            g, i = u // IMAGES, u % IMAGES
+            features = slice(g * K_PASS, (g + 1) * K_PASS)
+            x_sb = x_pool.tile([P, HALVES, K_PASS], BF16, name="x_sb")
+            nc.sync.dma_start(out=x_sb[:], in_=x_view[:, i * HALVES : (i + 1) * HALVES, features])
+            if i == 0:
+                w_sb = w_pool.tile([P, OUT_FEATURES], U32, name="w_sb", align_bytes=64)
+                nc.sync.dma_start(out=w_sb[:].bitcast(I32), in_=w_view[g].bitcast(I32))
+                weights[g] = w_sb
+            if on_vector(u):
+                transpose(u, x_sb)
+            else:
+                x_mid = x_pool.tile([P, K_PASS], BF16, name="x_mid")
+                nc.sync.dma_start(out=x_mid[:], in_=X[i, P // 2 : P // 2 + P, features])
+                sums_on_tensor(u, x_sb, x_mid)
+
+        def sums_on_tensor(u, x_sb, x_mid):
+            row = GRID_COLS
+            ax = ax_pool.tile([P, NODES, PACK], BF16, name="ax", align_bytes=64)
+            for h in range(HALVES):
+                sums = work_pool.tile([P, PACK, P], F32, name="sums", tag="work")
+                for t in range(PACK):
+                    k_cols = slice(t, K_PASS, PACK)
+                    if h == 0:
                         nc.tensor.matmul(
-                            out=sums[:, t, :],
-                            lhsT=x_sb[:, i * HALVES + h, k_cols],
-                            rhs=onto_own_block,
+                            out=sums[:, t, 0 : P - row],
+                            lhsT=x_sb[:, 0, k_cols],
+                            rhs=adjacency[:, 0 : P - row],
                             start=True,
-                            stop=False,
+                            stop=True,
                         )
-                        if h == 0:
-                            nc.tensor.matmul(
-                                out=sums[:, t, P - GRID_COLS : P],
-                                lhsT=x_sb[:, i * HALVES + 1, k_cols],
-                                rhs=onto_row_before,
-                                start=False,
-                                stop=True,
-                            )
-                        else:
-                            nc.tensor.matmul(
-                                out=sums[:, t, 0:GRID_COLS],
-                                lhsT=x_sb[:, i * HALVES, k_cols],
-                                rhs=onto_row_after,
-                                start=False,
-                                stop=True,
-                            )
-                    nc.scalar.copy(out=ax[:, i, h * P : (h + 1) * P, :], in_=sums[:].rearrange("p t n -> p n t"))
+                        nc.tensor.matmul(
+                            out=sums[:, t, P - row : P],
+                            lhsT=x_mid[:, k_cols],
+                            rhs=adjacency[:, P // 2 - row : P // 2],
+                            start=True,
+                            stop=True,
+                        )
+                    else:
+                        nc.tensor.matmul(
+                            out=sums[:, t, 0:row],
+                            lhsT=x_mid[:, k_cols],
+                            rhs=adjacency[:, P // 2 : P // 2 + row],
+                            start=True,
+                            stop=True,
+                        )
+                        nc.tensor.matmul(
+                            out=sums[:, t, row:P],
+                            lhsT=x_sb[:, 1, k_cols],
+                            rhs=adjacency[:, row:P],
+                            start=True,
+                            stop=True,
+                        )
+                nc.scalar.copy(out=ax[:, h * P : (h + 1) * P, :], in_=sums[:].rearrange("p t n -> p n t"))
+            totals[u] = ax
 
-        def first_adds_on_vector(g, x_sb):
+        def transpose(u, x_sb):
             x_words = x_sb[:].bitcast(F32)
-            turn = g % TENSOR_EVERY // 2
-            above = shifted_down[turn]
-            triple = triples[turn]
-            pair = sum_pool.tile([P, IMAGES, NODES, PACK], F32, name="pair")
-            sides = sum_pool.tile([P, IMAGES, GRID_ROWS, GRID_COLS * PACK], F32, name="sides")
-            banks = []
-            for i in range(IMAGES):
-                xt = work_pool.tile([P, 2, NODES], F32, name="xt", tag="work")
-                for u in range(2):
-                    for h in range(HALVES):
-                        nc.tensor.transpose(
-                            out=xt[:, u, h * P : (h + 1) * P],
-                            in_=x_words[:, i * HALVES + h, u : K_PASS // 2 : 2],
-                            identity=ident_words[:],
-                        )
-                nc.scalar.copy(
-                    out=above[:, i, GRID_COLS:, :].bitcast(F32), in_=xt[:].rearrange("p u n -> p n u")
-                )
-                nc.scalar.copy(
-                    out=pair[:, i, NODES - GRID_COLS :, :], in_=above[:, i, NODES - GRID_COLS : NODES, :]
-                )
-                banks.append(xt[:].bitcast(BF16).rearrange("p u (n e) -> p n u e", e=2))
-            for i in range(IMAGES):
-                nc.vector.tensor_tensor(
-                    out=pair[:, i, 0 : NODES - GRID_COLS, :].rearrange("p n (u e) -> p n u e", e=2),
-                    in0=banks[i][:, GRID_COLS:, :, :],
-                    in1=above[:, i, 0 : NODES - GRID_COLS, :].rearrange("p n (u e) -> p n u e", e=2),
-                    op=ADD,
-                )
-            for i in range(IMAGES):
-                nc.vector.tensor_tensor(
-                    out=triple[:, i, :, PACK : (GRID_COLS + 1) * PACK].rearrange(
-                        "p r (c u e) -> p r c u e", u=2, e=2
-                    ),
-                    in0=banks[i].rearrange("p (r c) u e -> p r c u e", c=GRID_COLS),
-                    in1=pair[:, i, :, :].rearrange("p (r c) (u e) -> p r c u e", c=GRID_COLS, e=2),
-                    op=ADD,
-                )
-            for i in range(IMAGES):
-                nc.gpsimd.tensor_tensor(
-                    out=sides[:, i, :, :],
-                    in0=triple[:, i, :, 0 : GRID_COLS * PACK],
-                    in1=triple[:, i, :, 2 * PACK :],
-                    op=ADD,
-                )
-            return pair, sides
-
-        def last_add_on_vector(pair, sides, ax):
-            for i in range(IMAGES):
-                nc.vector.tensor_tensor(
-                    out=ax[:, i, :, :].rearrange("p n t -> p (n t)"),
-                    in0=sides[:, i, :, :].rearrange("p r w -> p (r w)"),
-                    in1=pair[:, i, :, :].rearrange("p n t -> p (n t)"),
-                    op=ADD,
-                )
-
-        def multiply(g, ax, w_sb):
-            codes = ax_pool.tile([P, IMAGES * NODES], U32, name="codes", align_bytes=64)
-            scales = ax_pool.tile([P, IMAGES * NODES], U8, name="scales", align_bytes=64)
-            nc.vector.quantize_mx(
-                out=codes[:].bitcast(FP8X4), scales=scales[:], in_=ax[:].rearrange("p i n t -> p (i n t)")
+            xt = work_pool.tile([P, 2, NODES], F32, name="xt", tag="work")
+            for u2 in range(2):
+                for h in range(HALVES):
+                    nc.tensor.transpose(
+                        out=xt[:, u2, h * P : (h + 1) * P],
+                        in_=x_words[:, h, u2 : K_PASS // 2 : 2],
+                        identity=ident_words[:],
+                    )
+            x_copy = copy_pool.tile([P, NODES, PACK], BF16, name="x_copy")
+            nc.scalar.copy(out=x_copy[:].bitcast(F32), in_=xt[:].rearrange("p u n -> p n u"))
+            pair = pair_pool.tile([P, NODES, PACK], F32, name="pair")
+            nc.scalar.copy(
+                out=pair[:].rearrange("p (r c) t -> p r (c t)", c=GRID_COLS)[:, 0 : GRID_ROWS : GRID_ROWS - 1, :],
+                in_=x_copy[:].rearrange("p (r c) t -> p r (c t)", c=GRID_COLS)[:, 1 : GRID_ROWS - 1 : GRID_ROWS - 3, :],
             )
-            for m in range(IMAGES * HALVES):
-                cols = slice(m * P, (m + 1) * P)
+            values[u] = xt[:].bitcast(BF16).rearrange("p u (n e) -> p n u e", e=2)
+            copies[u] = x_copy
+            pairs[u] = pair
+
+        def add_rows(u):
+            nc.vector.tensor_tensor(
+                out=lanes(pairs[u][:, GRID_COLS : NODES - GRID_COLS, :]),
+                in0=values[u][:, 2 * GRID_COLS :, :, :],
+                in1=lanes(copies[u][:, 0 : NODES - 2 * GRID_COLS, :]),
+                op=ADD,
+            )
+
+        def add_own_row(u):
+            nc.vector.tensor_tensor(
+                out=triples[u % 3][:, :, PACK : (GRID_COLS + 1) * PACK].rearrange(
+                    "p r (c u e) -> p r c u e", u=2, e=2
+                ),
+                in0=values[u].rearrange("p (r c) u e -> p r c u e", c=GRID_COLS),
+                in1=pairs[u][:].rearrange("p (r c) (u e) -> p r c u e", c=GRID_COLS, e=2),
+                op=ADD,
+            )
+
+        def add_columns(u):
+            side = sides_pool.tile([P, GRID_ROWS, GRID_COLS * PACK], F32, name="side")
+            nc.vector.tensor_tensor(
+                out=side[:],
+                in0=triples[u % 3][:, :, 0 : GRID_COLS * PACK],
+                in1=triples[u % 3][:, :, 2 * PACK :],
+                op=ADD,
+            )
+            sides[u] = side
+
+        def add_up(u):
+            ax = ax_pool.tile([P, NODES, PACK], BF16, name="ax", align_bytes=64)
+            nc.vector.tensor_tensor(
+                out=ax[:].rearrange("p n t -> p (n t)"),
+                in0=sides[u][:].rearrange("p r w -> p (r w)"),
+                in1=pairs[u][:].rearrange("p n t -> p (n t)"),
+                op=ADD,
+            )
+            totals[u] = ax
+
+        def multiply(u):
+            g, i = u // IMAGES, u % IMAGES
+            codes = mx_pool.tile([P, NODES], U32, name="codes", align_bytes=64)
+            scales = mx_pool.tile([P, NODES], U8, name="scales", align_bytes=64)
+            nc.vector.quantize_mx(
+                out=codes[:].bitcast(FP8X4), scales=scales[:], in_=totals[u][:].rearrange("p n t -> p (n t)")
+            )
+            for h in range(HALVES):
+                cols = slice(h * P, (h + 1) * P)
                 nc.tensor.matmul_mx(
-                    out=acc[m][:],
+                    out=acc[i * HALVES + h][:],
                     lhsT=codes[:, cols].bitcast(FP8X4),
                     lhsT_scale=scales[:, cols],
-                    rhs=w_sb[:].bitcast(FP8X4),
+                    rhs=weights[g][:].bitcast(FP8X4),
                     rhs_scale=w_scales[:, g, :],
                     start=(g == 0),
                     stop=(g == GROUPS - 1),
                 )
 
-        begun = {}
-        for step in range(GROUPS + LAG):
-            if step < GROUPS:
-                g = step
-                x_sb, w_sb = load(g)
-                if g == 0:
-                    for quadrant in range(4):
-                        nc.sync.dma_start(
-                            out=w_scales[32 * quadrant : 32 * quadrant + 4, :, :].bitcast(I32),
-                            in_=s_view[4 * quadrant : 4 * quadrant + 4, :, :].bitcast(I32),
-                        )
-                if g % TENSOR_EVERY == TENSOR_FIRST:
-                    ax = ax_pool.tile([P, IMAGES, NODES, PACK], BF16, name="ax", align_bytes=64)
-                    sums_on_tensor(x_sb, ax)
-                    begun[g] = (w_sb, ax, None, None)
-                else:
-                    pair, sides = first_adds_on_vector(g, x_sb)
-                    begun[g] = (w_sb, None, pair, sides)
-            if step >= LAG:
-                g = step - LAG
-                w_sb, ax, pair, sides = begun[g]
-                if ax is None:
-                    ax = ax_pool.tile([P, IMAGES, NODES, PACK], BF16, name="ax", align_bytes=64)
-                    last_add_on_vector(pair, sides, ax)
-                multiply(g, ax, w_sb)
+        for step in range(UNITS + 4):
+            if step < UNITS:
+                prepare(step)
+            if step == 0:
+                for quadrant in range(4):
+                    nc.sync.dma_start(
+                        out=w_scales[32 * quadrant : 32 * quadrant + 4, :, :].bitcast(I32),
+                        in_=s_view[4 * quadrant : 4 * quadrant + 4, :, :].bitcast(I32),
+                    )
+            if on_vector(step):
+                add_rows(step)
+            if on_vector(step - 1):
+                add_own_row(step - 1)
+            if on_vector(step - 2):
+                add_columns(step - 2)
+            if on_vector(step - 3):
+                add_up(step - 3)
+            if step >= 4:
+                multiply(step - 4)
 
         for m in range(IMAGES * HALVES):
             result = res_pool.tile([P, OUT_FEATURES], F32, name="result")
             nc.vector.tensor_tensor(out=result[:], in0=acc[m][:], in1=bias[:], op=ADD)
-            nc.sync.dma_start(out=out.rearrange("i (h p) n -> (i h) p n", p=P)[m], in_=result[:])
+            nc.sync.dma_start(out=out_view[m], in_=result[:])

@@ -47,9 +47,10 @@ def tile_graphconvlayer_k_kernel(tc, X, Wm_words, Wm_scales, b, H, W, out):
         const = ctx.enter_context(tc.tile_pool(name="const", bufs=1))
         x_pool = ctx.enter_context(tc.tile_pool(name="x", bufs=6))
         w_pool = ctx.enter_context(tc.tile_pool(name="w", bufs=6))
-        copy_pool = ctx.enter_context(tc.tile_pool(name="copies", bufs=3))
+        copy_pool = ctx.enter_context(tc.tile_pool(name="copies", bufs=4))
         pair_pool = ctx.enter_context(tc.tile_pool(name="pairs", bufs=6))
-        sides_pool = ctx.enter_context(tc.tile_pool(name="sides", bufs=3))
+        triple_pool = ctx.enter_context(tc.tile_pool(name="triples", bufs=3))
+        sides_pool = ctx.enter_context(tc.tile_pool(name="sides", bufs=4))
         ax_pool = ctx.enter_context(tc.tile_pool(name="ax", bufs=7))
         mx_pool = ctx.enter_context(tc.tile_pool(name="mx", bufs=3))
         res_pool = ctx.enter_context(tc.tile_pool(name="res", bufs=2))
@@ -84,27 +85,17 @@ def tile_graphconvlayer_k_kernel(tc, X, Wm_words, Wm_scales, b, H, W, out):
             )
         adjacency = adjacency_grid[:].rearrange("p r c -> p (r c)")
 
-        triples = [
-            const.tile([P, GRID_ROWS, (GRID_COLS + 2) * PACK], F32, name="triples%d" % n) for n in range(3)
-        ]
-        for fixed in triples:
-            nc.vector.memset(fixed[:, :, 0:PACK], 0.0)
-            nc.vector.memset(fixed[:, :, (GRID_COLS + 1) * PACK :], 0.0)
-
         acc = [acc_pool.tile([P, OUT_FEATURES], F32, name="acc%d" % m) for m in range(IMAGES * HALVES)]
 
         weights = {}
         values = {}
-        copies = {}
         pairs = {}
+        triples = {}
         sides = {}
         totals = {}
 
         def on_vector(u):
             return 0 <= u < UNITS and u % TENSOR_PERIOD not in TENSOR_TURNS
-
-        def lanes(ap):
-            return ap.rearrange("p n (u e) -> p n u e", e=2)
 
         def prepare(u):
             g, i = u // IMAGES, u % IMAGES
@@ -179,44 +170,47 @@ def tile_graphconvlayer_k_kernel(tc, X, Wm_words, Wm_scales, b, H, W, out):
                 out=pair[:].rearrange("p (r c) t -> p r (c t)", c=GRID_COLS)[:, 0 : GRID_ROWS : GRID_ROWS - 1, :],
                 in_=x_copy[:].rearrange("p (r c) t -> p r (c t)", c=GRID_COLS)[:, 1 : GRID_ROWS - 1 : GRID_ROWS - 3, :],
             )
-            values[u] = xt[:].bitcast(BF16).rearrange("p u (n e) -> p n u e", e=2)
-            copies[u] = x_copy
+            values[u] = x_copy
             pairs[u] = pair
 
         def add_rows(u):
             nc.vector.tensor_tensor(
-                out=lanes(pairs[u][:, GRID_COLS : NODES - GRID_COLS, :]),
-                in0=values[u][:, 2 * GRID_COLS :, :, :],
-                in1=lanes(copies[u][:, 0 : NODES - 2 * GRID_COLS, :]),
+                out=pairs[u][:, GRID_COLS : NODES - GRID_COLS, :],
+                in0=values[u][:, 2 * GRID_COLS :, :],
+                in1=values[u][:, 0 : NODES - 2 * GRID_COLS, :],
                 op=ADD,
             )
 
         def add_own_row(u):
+            triple = triple_pool.tile([P, NODES, PACK], F32, name="triple")
             nc.vector.tensor_tensor(
-                out=triples[u % 3][:, :, PACK : (GRID_COLS + 1) * PACK].rearrange(
-                    "p r (c u e) -> p r c u e", u=2, e=2
-                ),
-                in0=values[u].rearrange("p (r c) u e -> p r c u e", c=GRID_COLS),
-                in1=pairs[u][:].rearrange("p (r c) (u e) -> p r c u e", c=GRID_COLS, e=2),
+                out=triple[:].rearrange("p (c r) t -> p c r t", r=GRID_ROWS),
+                in0=pairs[u][:].rearrange("p (r c) t -> p c r t", c=GRID_COLS),
+                in1=values[u][:].rearrange("p (r c) t -> p c r t", c=GRID_COLS),
                 op=ADD,
             )
+            side = sides_pool.tile([P, NODES, PACK], F32, name="side")
+            nc.scalar.copy(
+                out=side[:].rearrange("p (c r) t -> p c (r t)", r=GRID_ROWS)[:, 0 : GRID_COLS : GRID_COLS - 1, :],
+                in_=triple[:].rearrange("p (c r) t -> p c (r t)", r=GRID_ROWS)[:, 1 : GRID_COLS - 1 : GRID_COLS - 3, :],
+            )
+            triples[u] = triple
+            sides[u] = side
 
         def add_columns(u):
-            side = sides_pool.tile([P, GRID_ROWS, GRID_COLS * PACK], F32, name="side")
             nc.vector.tensor_tensor(
-                out=side[:],
-                in0=triples[u % 3][:, :, 0 : GRID_COLS * PACK],
-                in1=triples[u % 3][:, :, 2 * PACK :],
+                out=sides[u][:, GRID_ROWS : NODES - GRID_ROWS, :],
+                in0=triples[u][:, 0 : NODES - 2 * GRID_ROWS, :],
+                in1=triples[u][:, 2 * GRID_ROWS :, :],
                 op=ADD,
             )
-            sides[u] = side
 
         def add_up(u):
             ax = ax_pool.tile([P, NODES, PACK], BF16, name="ax", align_bytes=64)
             nc.vector.tensor_tensor(
-                out=ax[:].rearrange("p n t -> p (n t)"),
-                in0=sides[u][:].rearrange("p r w -> p (r w)"),
-                in1=pairs[u][:].rearrange("p n t -> p (n t)"),
+                out=ax[:].rearrange("p (r c) t -> p r c t", c=GRID_COLS),
+                in0=sides[u][:].rearrange("p (c r) t -> p r c t", r=GRID_ROWS),
+                in1=pairs[u][:].rearrange("p (r c) t -> p r c t", c=GRID_COLS),
                 op=ADD,
             )
             totals[u] = ax

@@ -32,6 +32,10 @@ TENSOR_PERIOD = 5
 TENSOR_TURNS = (2, 4)
 TENSOR_UNITS = len([u for u in range(UNITS) if u % TENSOR_PERIOD in TENSOR_TURNS])
 assert 10 * TENSOR_UNITS * 2 * P * P * NODES * PACK <= FLOPS
+VECTOR_UNITS = [u for u in range(UNITS) if u % TENSOR_PERIOD not in TENSOR_TURNS]
+
+GPSIMD_ROWS = 8
+LOADS_AHEAD = 6
 
 
 def tile_graphconvlayer_k_kernel(tc, X, Wm_words, Wm_scales, b, H, W, out):
@@ -45,13 +49,12 @@ def tile_graphconvlayer_k_kernel(tc, X, Wm_words, Wm_scales, b, H, W, out):
 
     with ExitStack() as ctx:
         const = ctx.enter_context(tc.tile_pool(name="const", bufs=1))
-        x_pool = ctx.enter_context(tc.tile_pool(name="x", bufs=6))
-        w_pool = ctx.enter_context(tc.tile_pool(name="w", bufs=6))
-        copy_pool = ctx.enter_context(tc.tile_pool(name="copies", bufs=4))
+        x_pool = ctx.enter_context(tc.tile_pool(name="x", bufs=LOADS_AHEAD + 3))
+        w_pool = ctx.enter_context(tc.tile_pool(name="w", bufs=10))
+        copy_pool = ctx.enter_context(tc.tile_pool(name="copies", bufs=3))
         pair_pool = ctx.enter_context(tc.tile_pool(name="pairs", bufs=6))
-        triple_pool = ctx.enter_context(tc.tile_pool(name="triples", bufs=3))
         sides_pool = ctx.enter_context(tc.tile_pool(name="sides", bufs=4))
-        ax_pool = ctx.enter_context(tc.tile_pool(name="ax", bufs=7))
+        ax_pool = ctx.enter_context(tc.tile_pool(name="ax", bufs=10))
         mx_pool = ctx.enter_context(tc.tile_pool(name="mx", bufs=3))
         res_pool = ctx.enter_context(tc.tile_pool(name="res", bufs=2))
         acc_pool = ctx.enter_context(tc.psum_pool(name="acc", bufs=1))
@@ -85,19 +88,27 @@ def tile_graphconvlayer_k_kernel(tc, X, Wm_words, Wm_scales, b, H, W, out):
             )
         adjacency = adjacency_grid[:].rearrange("p r c -> p (r c)")
 
+        triples = [
+            const.tile([P, GRID_ROWS, (GRID_COLS + 2) * PACK], F32, name="triples%d" % n) for n in range(3)
+        ]
+        for fixed in triples:
+            nc.vector.memset(fixed[:, :, 0:PACK], 0.0)
+            nc.vector.memset(fixed[:, :, (GRID_COLS + 1) * PACK :], 0.0)
+
         acc = [acc_pool.tile([P, OUT_FEATURES], F32, name="acc%d" % m) for m in range(IMAGES * HALVES)]
 
+        loaded = {}
         weights = {}
         values = {}
+        copies = {}
         pairs = {}
-        triples = {}
         sides = {}
         totals = {}
 
-        def on_vector(u):
-            return 0 <= u < UNITS and u % TENSOR_PERIOD not in TENSOR_TURNS
+        def lanes(ap):
+            return ap.rearrange("p n (u e) -> p n u e", e=2)
 
-        def prepare(u):
+        def load(u):
             g, i = u // IMAGES, u % IMAGES
             features = slice(g * K_PASS, (g + 1) * K_PASS)
             x_sb = x_pool.tile([P, HALVES, K_PASS], BF16, name="x_sb")
@@ -106,11 +117,17 @@ def tile_graphconvlayer_k_kernel(tc, X, Wm_words, Wm_scales, b, H, W, out):
                 w_sb = w_pool.tile([P, OUT_FEATURES], U32, name="w_sb", align_bytes=64)
                 nc.sync.dma_start(out=w_sb[:].bitcast(I32), in_=w_view[g].bitcast(I32))
                 weights[g] = w_sb
-            if on_vector(u):
-                transpose(u, x_sb)
-            else:
+            x_mid = None
+            if u not in VECTOR_UNITS:
                 x_mid = x_pool.tile([P, K_PASS], BF16, name="x_mid")
                 nc.sync.dma_start(out=x_mid[:], in_=X[i, P // 2 : P // 2 + P, features])
+            loaded[u] = (x_sb, x_mid)
+
+        def prepare(u):
+            x_sb, x_mid = loaded[u]
+            if u in VECTOR_UNITS:
+                transpose(u, x_sb)
+            else:
                 sums_on_tensor(u, x_sb, x_mid)
 
         def sums_on_tensor(u, x_sb, x_mid):
@@ -170,47 +187,42 @@ def tile_graphconvlayer_k_kernel(tc, X, Wm_words, Wm_scales, b, H, W, out):
                 out=pair[:].rearrange("p (r c) t -> p r (c t)", c=GRID_COLS)[:, 0 : GRID_ROWS : GRID_ROWS - 1, :],
                 in_=x_copy[:].rearrange("p (r c) t -> p r (c t)", c=GRID_COLS)[:, 1 : GRID_ROWS - 1 : GRID_ROWS - 3, :],
             )
-            values[u] = x_copy
+            values[u] = xt[:].bitcast(BF16).rearrange("p u (n e) -> p n u e", e=2)
+            copies[u] = x_copy
             pairs[u] = pair
 
         def add_rows(u):
             nc.vector.tensor_tensor(
-                out=pairs[u][:, GRID_COLS : NODES - GRID_COLS, :],
-                in0=values[u][:, 2 * GRID_COLS :, :],
-                in1=values[u][:, 0 : NODES - 2 * GRID_COLS, :],
+                out=lanes(pairs[u][:, GRID_COLS : NODES - GRID_COLS, :]),
+                in0=values[u][:, 2 * GRID_COLS :, :, :],
+                in1=lanes(copies[u][:, 0 : NODES - 2 * GRID_COLS, :]),
                 op=ADD,
             )
 
         def add_own_row(u):
-            triple = triple_pool.tile([P, NODES, PACK], F32, name="triple")
             nc.vector.tensor_tensor(
-                out=triple[:].rearrange("p (c r) t -> p c r t", r=GRID_ROWS),
-                in0=pairs[u][:].rearrange("p (r c) t -> p c r t", c=GRID_COLS),
-                in1=values[u][:].rearrange("p (r c) t -> p c r t", c=GRID_COLS),
+                out=triples[u % 3][:, :, PACK : (GRID_COLS + 1) * PACK].rearrange(
+                    "p r (c u e) -> p r c u e", u=2, e=2
+                ),
+                in0=values[u].rearrange("p (r c) u e -> p r c u e", c=GRID_COLS),
+                in1=pairs[u][:].rearrange("p (r c) (u e) -> p r c u e", c=GRID_COLS, e=2),
                 op=ADD,
             )
-            side = sides_pool.tile([P, NODES, PACK], F32, name="side")
-            nc.scalar.copy(
-                out=side[:].rearrange("p (c r) t -> p c (r t)", r=GRID_ROWS)[:, 0 : GRID_COLS : GRID_COLS - 1, :],
-                in_=triple[:].rearrange("p (c r) t -> p c (r t)", r=GRID_ROWS)[:, 1 : GRID_COLS - 1 : GRID_COLS - 3, :],
-            )
-            triples[u] = triple
-            sides[u] = side
 
-        def add_columns(u):
-            nc.vector.tensor_tensor(
-                out=sides[u][:, GRID_ROWS : NODES - GRID_ROWS, :],
-                in0=triples[u][:, 0 : NODES - 2 * GRID_ROWS, :],
-                in1=triples[u][:, 2 * GRID_ROWS :, :],
+        def add_columns(engine, u, rows):
+            engine.tensor_tensor(
+                out=sides[u][:, rows, :],
+                in0=triples[u % 3][:, rows, 0 : GRID_COLS * PACK],
+                in1=triples[u % 3][:, rows, 2 * PACK :],
                 op=ADD,
             )
 
         def add_up(u):
             ax = ax_pool.tile([P, NODES, PACK], BF16, name="ax", align_bytes=64)
             nc.vector.tensor_tensor(
-                out=ax[:].rearrange("p (r c) t -> p r c t", c=GRID_COLS),
-                in0=sides[u][:].rearrange("p (c r) t -> p r c t", r=GRID_ROWS),
-                in1=pairs[u][:].rearrange("p (r c) t -> p r c t", c=GRID_COLS),
+                out=ax[:].rearrange("p n t -> p (n t)"),
+                in0=sides[u][:].rearrange("p r w -> p (r w)"),
+                in1=pairs[u][:].rearrange("p n t -> p (n t)"),
                 op=ADD,
             )
             totals[u] = ax
@@ -234,25 +246,41 @@ def tile_graphconvlayer_k_kernel(tc, X, Wm_words, Wm_scales, b, H, W, out):
                     stop=(g == GROUPS - 1),
                 )
 
-        for step in range(UNITS + 4):
-            if step < UNITS:
-                prepare(step)
-            if step == 0:
-                for quadrant in range(4):
-                    nc.sync.dma_start(
-                        out=w_scales[32 * quadrant : 32 * quadrant + 4, :, :].bitcast(I32),
-                        in_=s_view[4 * quadrant : 4 * quadrant + 4, :, :].bitcast(I32),
-                    )
-            if on_vector(step):
-                add_rows(step)
-            if on_vector(step - 1):
-                add_own_row(step - 1)
-            if on_vector(step - 2):
-                add_columns(step - 2)
-            if on_vector(step - 3):
-                add_up(step - 3)
-            if step >= 4:
-                multiply(step - 4)
+        steps = len(VECTOR_UNITS)
+        loads_written = 0
+        prepared = 0
+        multiplied = 0
+        with tc.manual_schedule():
+            for step in range(steps + 4):
+                upto = VECTOR_UNITS[step + 1] + 1 if step + 1 < steps else UNITS
+                for u in range(loads_written, min(upto + LOADS_AHEAD, UNITS)):
+                    load(u)
+                    if u == 1:
+                        for quadrant in range(4):
+                            nc.sync.dma_start(
+                                out=w_scales[32 * quadrant : 32 * quadrant + 4, :, :].bitcast(I32),
+                                in_=s_view[4 * quadrant : 4 * quadrant + 4, :, :].bitcast(I32),
+                            )
+                loads_written = max(loads_written, min(upto + LOADS_AHEAD, UNITS))
+                for u in sorted(range(prepared, upto), key=lambda u: u not in VECTOR_UNITS):
+                    prepare(u)
+                prepared = upto
+
+                if step < steps:
+                    add_rows(VECTOR_UNITS[step])
+                if 0 <= step - 1 < steps:
+                    u = VECTOR_UNITS[step - 1]
+                    add_own_row(u)
+                    sides[u] = sides_pool.tile([P, GRID_ROWS, GRID_COLS * PACK], F32, name="side")
+                    add_columns(nc.gpsimd, u, slice(0, GPSIMD_ROWS))
+                if 0 <= step - 2 < steps:
+                    add_columns(nc.vector, VECTOR_UNITS[step - 2], slice(GPSIMD_ROWS, GRID_ROWS))
+                if 0 <= step - 3 < steps:
+                    add_up(VECTOR_UNITS[step - 3])
+                if 0 <= step - 4 < steps:
+                    for u in range(multiplied, VECTOR_UNITS[step - 4] + 1):
+                        multiply(u)
+                    multiplied = VECTOR_UNITS[step - 4] + 1
 
         for m in range(IMAGES * HALVES):
             result = res_pool.tile([P, OUT_FEATURES], F32, name="result")

@@ -34,7 +34,6 @@ TENSOR_UNITS = len([u for u in range(UNITS) if u % TENSOR_PERIOD in TENSOR_TURNS
 assert 10 * TENSOR_UNITS * 2 * P * P * NODES * PACK <= FLOPS
 VECTOR_UNITS = [u for u in range(UNITS) if u % TENSOR_PERIOD not in TENSOR_TURNS]
 
-GPSIMD_ROWS = 8
 LOADS_AHEAD = 6
 
 
@@ -53,7 +52,8 @@ def tile_graphconvlayer_k_kernel(tc, X, Wm_words, Wm_scales, b, H, W, out):
         w_pool = ctx.enter_context(tc.tile_pool(name="w", bufs=10))
         copy_pool = ctx.enter_context(tc.tile_pool(name="copies", bufs=3))
         pair_pool = ctx.enter_context(tc.tile_pool(name="pairs", bufs=6))
-        sides_pool = ctx.enter_context(tc.tile_pool(name="sides", bufs=4))
+        triple_pool = ctx.enter_context(tc.tile_pool(name="triples", bufs=3))
+        sides_pool = ctx.enter_context(tc.tile_pool(name="sides", bufs=1))
         ax_pool = ctx.enter_context(tc.tile_pool(name="ax", bufs=10))
         mx_pool = ctx.enter_context(tc.tile_pool(name="mx", bufs=3))
         res_pool = ctx.enter_context(tc.tile_pool(name="res", bufs=2))
@@ -88,13 +88,6 @@ def tile_graphconvlayer_k_kernel(tc, X, Wm_words, Wm_scales, b, H, W, out):
             )
         adjacency = adjacency_grid[:].rearrange("p r c -> p (r c)")
 
-        triples = [
-            const.tile([P, GRID_ROWS, (GRID_COLS + 2) * PACK], F32, name="triples%d" % n) for n in range(3)
-        ]
-        for fixed in triples:
-            nc.vector.memset(fixed[:, :, 0:PACK], 0.0)
-            nc.vector.memset(fixed[:, :, (GRID_COLS + 1) * PACK :], 0.0)
-
         acc = [acc_pool.tile([P, OUT_FEATURES], F32, name="acc%d" % m) for m in range(IMAGES * HALVES)]
 
         loaded = {}
@@ -102,6 +95,7 @@ def tile_graphconvlayer_k_kernel(tc, X, Wm_words, Wm_scales, b, H, W, out):
         values = {}
         copies = {}
         pairs = {}
+        triples = {}
         sides = {}
         totals = {}
 
@@ -200,22 +194,24 @@ def tile_graphconvlayer_k_kernel(tc, X, Wm_words, Wm_scales, b, H, W, out):
             )
 
         def add_own_row(u):
-            nc.vector.tensor_tensor(
-                out=triples[u % 3][:, :, PACK : (GRID_COLS + 1) * PACK].rearrange(
-                    "p r (c u e) -> p r c u e", u=2, e=2
-                ),
-                in0=values[u].rearrange("p (r c) u e -> p r c u e", c=GRID_COLS),
-                in1=pairs[u][:].rearrange("p (r c) (u e) -> p r c u e", c=GRID_COLS, e=2),
-                op=ADD,
-            )
+            triple = triple_pool.tile([P, NODES, PACK], F32, name="triple")
+            nc.vector.tensor_tensor(out=lanes(triple[:]), in0=values[u], in1=lanes(pairs[u][:]), op=ADD)
+            triples[u] = triple
 
-        def add_columns(engine, u, rows):
-            engine.tensor_tensor(
-                out=sides[u][:, rows, :],
-                in0=triples[u % 3][:, rows, 0 : GRID_COLS * PACK],
-                in1=triples[u % 3][:, rows, 2 * PACK :],
+        def add_columns(u):
+            side = sides_pool.tile([P, GRID_ROWS, GRID_COLS * PACK], F32, name="side")
+            triple = triples[u][:].rearrange("p (r c) t -> p r (c t)", c=GRID_COLS)
+            nc.gpsimd.tensor_tensor(
+                out=side[:, :, PACK : (GRID_COLS - 1) * PACK],
+                in0=triple[:, :, 0 : (GRID_COLS - 2) * PACK],
+                in1=triple[:, :, 2 * PACK :],
                 op=ADD,
             )
+            nc.scalar.copy(
+                out=side[:].rearrange("p r (c t) -> p r c t", t=PACK)[:, :, 0 : GRID_COLS : GRID_COLS - 1, :],
+                in_=triple.rearrange("p r (c t) -> p r c t", t=PACK)[:, :, 1 : GRID_COLS - 1 : GRID_COLS - 3, :],
+            )
+            sides[u] = side
 
         def add_up(u):
             ax = ax_pool.tile([P, NODES, PACK], BF16, name="ax", align_bytes=64)
@@ -266,21 +262,18 @@ def tile_graphconvlayer_k_kernel(tc, X, Wm_words, Wm_scales, b, H, W, out):
                     prepare(u)
                 prepared = upto
 
-                if step < steps:
-                    add_rows(VECTOR_UNITS[step])
-                if 0 <= step - 1 < steps:
-                    u = VECTOR_UNITS[step - 1]
-                    add_own_row(u)
-                    sides[u] = sides_pool.tile([P, GRID_ROWS, GRID_COLS * PACK], F32, name="side")
-                    add_columns(nc.gpsimd, u, slice(0, GPSIMD_ROWS))
-                if 0 <= step - 2 < steps:
-                    add_columns(nc.vector, VECTOR_UNITS[step - 2], slice(GPSIMD_ROWS, GRID_ROWS))
-                if 0 <= step - 3 < steps:
-                    add_up(VECTOR_UNITS[step - 3])
                 if 0 <= step - 4 < steps:
                     for u in range(multiplied, VECTOR_UNITS[step - 4] + 1):
                         multiply(u)
                     multiplied = VECTOR_UNITS[step - 4] + 1
+                if 0 <= step - 3 < steps:
+                    add_up(VECTOR_UNITS[step - 3])
+                if step < steps:
+                    add_rows(VECTOR_UNITS[step])
+                if 0 <= step - 1 < steps:
+                    add_own_row(VECTOR_UNITS[step - 1])
+                if 0 <= step - 2 < steps:
+                    add_columns(VECTOR_UNITS[step - 2])
 
         for m in range(IMAGES * HALVES):
             result = res_pool.tile([P, OUT_FEATURES], F32, name="result")

@@ -23,18 +23,24 @@ BLOCK_ROWS = P // GRID_COLS
 FEATURES = 16384
 OUT_FEATURES = 512
 GROUPS = FEATURES // K_PASS
-UNITS = GROUPS * IMAGES
 OFFSETS = [(-1, 0), (1, 0), (0, -1), (0, 1), (-1, -1), (-1, 1), (1, -1), (1, 1)]
 
 FLOPS = 2 * IMAGES * NODES * FEATURES * OUT_FEATURES
 
 TENSOR_PERIOD = 5
 TENSOR_TURNS = (2, 4)
-TENSOR_UNITS = len([u for u in range(UNITS) if u % TENSOR_PERIOD in TENSOR_TURNS])
-assert 10 * TENSOR_UNITS * 2 * P * P * NODES * PACK <= FLOPS
-VECTOR_UNITS = [u for u in range(UNITS) if u % TENSOR_PERIOD not in TENSOR_TURNS]
+BATCHES = [(0, (0,)), (0, (1,))] + [(g, tuple(range(IMAGES))) for g in range(1, GROUPS)]
 
-LOADS_AHEAD = 6
+
+def on_tensor(batch):
+    return batch == (0, (1,)) or batch[0] % TENSOR_PERIOD in TENSOR_TURNS
+
+
+VECTOR_BATCHES = [k for k, batch in enumerate(BATCHES) if not on_tensor(batch)]
+TENSOR_UNITS = sum(len(batch[1]) for batch in BATCHES if on_tensor(batch))
+assert 10 * TENSOR_UNITS * 2 * P * P * NODES * PACK <= FLOPS
+
+LOADS_AHEAD = 3
 
 
 def tile_graphconvlayer_k_kernel(tc, X, Wm_words, Wm_scales, b, H, W, out):
@@ -42,23 +48,24 @@ def tile_graphconvlayer_k_kernel(tc, X, Wm_words, Wm_scales, b, H, W, out):
     assert H == GRID_ROWS and W == GRID_COLS
 
     x_view = X.rearrange("i (h p) k -> p (i h) k", p=P)
+    x_mid_view = X[:, P // 2 : P // 2 + P, :].rearrange("i p k -> p i k")
     w_view = Wm_words.rearrange("g p n t -> g p (n t)")
     s_view = Wm_scales.rearrange("g q n -> q g n")
     out_view = out.rearrange("i (h p) n -> (i h) p n", p=P)
 
     with ExitStack() as ctx:
         const = ctx.enter_context(tc.tile_pool(name="const", bufs=1))
-        x_pool = ctx.enter_context(tc.tile_pool(name="x", bufs=LOADS_AHEAD + 3))
-        w_pool = ctx.enter_context(tc.tile_pool(name="w", bufs=10))
-        copy_pool = ctx.enter_context(tc.tile_pool(name="copies", bufs=3))
-        pair_pool = ctx.enter_context(tc.tile_pool(name="pairs", bufs=6))
-        triple_pool = ctx.enter_context(tc.tile_pool(name="triples", bufs=3))
+        x_pool = ctx.enter_context(tc.tile_pool(name="x", bufs=LOADS_AHEAD + 4))
+        w_pool = ctx.enter_context(tc.tile_pool(name="w", bufs=LOADS_AHEAD + 9))
+        copy_pool = ctx.enter_context(tc.tile_pool(name="copies", bufs=2))
+        pair_pool = ctx.enter_context(tc.tile_pool(name="pairs", bufs=4))
+        triple_pool = ctx.enter_context(tc.tile_pool(name="triples", bufs=2))
         sides_pool = ctx.enter_context(tc.tile_pool(name="sides", bufs=1))
-        ax_pool = ctx.enter_context(tc.tile_pool(name="ax", bufs=10))
+        ax_pool = ctx.enter_context(tc.tile_pool(name="ax", bufs=6))
         mx_pool = ctx.enter_context(tc.tile_pool(name="mx", bufs=3))
         res_pool = ctx.enter_context(tc.tile_pool(name="res", bufs=2))
         acc_pool = ctx.enter_context(tc.psum_pool(name="acc", bufs=1))
-        work_pool = ctx.enter_context(tc.psum_pool(name="work", bufs=4))
+        work_pool = ctx.enter_context(tc.psum_pool(name="work", bufs=2))
 
         w_scales = const.tile([P, GROUPS, OUT_FEATURES], U8, align_bytes=64)
         nc.vector.memset(w_scales[:].rearrange("p g n -> p (g n)").bitcast(I32), 0)
@@ -102,178 +109,196 @@ def tile_graphconvlayer_k_kernel(tc, X, Wm_words, Wm_scales, b, H, W, out):
         def lanes(ap):
             return ap.rearrange("p n (u e) -> p n u e", e=2)
 
-        def load(u):
-            g, i = u // IMAGES, u % IMAGES
+        def images_of(k):
+            return BATCHES[k][1]
+
+        def used(k, tile):
+            return tile[:, 0 : len(images_of(k))]
+
+        def load(k):
+            g, images = BATCHES[k]
             features = slice(g * K_PASS, (g + 1) * K_PASS)
-            x_sb = x_pool.tile([P, HALVES, K_PASS], BF16, name="x_sb")
-            nc.sync.dma_start(out=x_sb[:], in_=x_view[:, i * HALVES : (i + 1) * HALVES, features])
-            if i == 0:
+            blocks = slice(images[0] * HALVES, (images[-1] + 1) * HALVES)
+            x_sb = x_pool.tile([P, IMAGES * HALVES, K_PASS], BF16, name="x_sb")
+            nc.sync.dma_start(out=x_sb[:, 0 : len(images) * HALVES, :], in_=x_view[:, blocks, features])
+            if g not in weights:
                 w_sb = w_pool.tile([P, OUT_FEATURES], U32, name="w_sb", align_bytes=64)
                 nc.sync.dma_start(out=w_sb[:].bitcast(I32), in_=w_view[g].bitcast(I32))
                 weights[g] = w_sb
             x_mid = None
-            if u not in VECTOR_UNITS:
-                x_mid = x_pool.tile([P, K_PASS], BF16, name="x_mid")
-                nc.sync.dma_start(out=x_mid[:], in_=X[i, P // 2 : P // 2 + P, features])
-            loaded[u] = (x_sb, x_mid)
+            if k not in VECTOR_BATCHES:
+                x_mid = x_pool.tile([P, IMAGES, K_PASS], BF16, name="x_mid")
+                nc.sync.dma_start(out=used(k, x_mid), in_=x_mid_view[:, images[0] : images[-1] + 1, features])
+            loaded[k] = (x_sb, x_mid)
 
-        def prepare(u):
-            x_sb, x_mid = loaded[u]
-            if u in VECTOR_UNITS:
-                transpose(u, x_sb)
-            else:
-                sums_on_tensor(u, x_sb, x_mid)
-
-        def sums_on_tensor(u, x_sb, x_mid):
+        def sums_on_tensor(k):
+            x_sb, x_mid = loaded[k]
             row = GRID_COLS
-            ax = ax_pool.tile([P, NODES, PACK], BF16, name="ax", align_bytes=64)
-            for h in range(HALVES):
-                sums = work_pool.tile([P, PACK, P], F32, name="sums", tag="work")
-                for t in range(PACK):
-                    k_cols = slice(t, K_PASS, PACK)
-                    if h == 0:
-                        nc.tensor.matmul(
-                            out=sums[:, t, 0 : P - row],
-                            lhsT=x_sb[:, 0, k_cols],
-                            rhs=adjacency[:, 0 : P - row],
-                            start=True,
-                            stop=True,
-                        )
-                        nc.tensor.matmul(
-                            out=sums[:, t, P - row : P],
-                            lhsT=x_mid[:, k_cols],
-                            rhs=adjacency[:, P // 2 - row : P // 2],
-                            start=True,
-                            stop=True,
-                        )
-                    else:
-                        nc.tensor.matmul(
-                            out=sums[:, t, 0:row],
-                            lhsT=x_mid[:, k_cols],
-                            rhs=adjacency[:, P // 2 : P // 2 + row],
-                            start=True,
-                            stop=True,
-                        )
-                        nc.tensor.matmul(
-                            out=sums[:, t, row:P],
-                            lhsT=x_sb[:, 1, k_cols],
-                            rhs=adjacency[:, row:P],
-                            start=True,
-                            stop=True,
-                        )
-                nc.scalar.copy(out=ax[:, h * P : (h + 1) * P, :], in_=sums[:].rearrange("p t n -> p n t"))
-            totals[u] = ax
-
-        def transpose(u, x_sb):
-            x_words = x_sb[:].bitcast(F32)
-            xt = work_pool.tile([P, 2, NODES], F32, name="xt", tag="work")
-            for u2 in range(2):
+            ax = ax_pool.tile([P, IMAGES, NODES, PACK], BF16, name="ax", align_bytes=64)
+            for j in range(len(images_of(k))):
                 for h in range(HALVES):
-                    nc.tensor.transpose(
-                        out=xt[:, u2, h * P : (h + 1) * P],
-                        in_=x_words[:, h, u2 : K_PASS // 2 : 2],
-                        identity=ident_words[:],
+                    sums = work_pool.tile([P, PACK, P], F32, name="sums")
+                    for t in range(PACK):
+                        k_cols = slice(t, K_PASS, PACK)
+                        if h == 0:
+                            parts = (
+                                (slice(0, P - row), x_sb[:, j * HALVES, k_cols], slice(0, P - row)),
+                                (slice(P - row, P), x_mid[:, j, k_cols], slice(P // 2 - row, P // 2)),
+                            )
+                        else:
+                            parts = (
+                                (slice(0, row), x_mid[:, j, k_cols], slice(P // 2, P // 2 + row)),
+                                (slice(row, P), x_sb[:, j * HALVES + 1, k_cols], slice(row, P)),
+                            )
+                        for nodes, values_in, neighbours in parts:
+                            nc.tensor.matmul(
+                                out=sums[:, t, nodes],
+                                lhsT=values_in,
+                                rhs=adjacency[:, neighbours],
+                                start=True,
+                                stop=True,
+                            )
+                    nc.scalar.copy(
+                        out=ax[:, j, h * P : (h + 1) * P, :], in_=sums[:].rearrange("p t n -> p n t")
                     )
-            x_copy = copy_pool.tile([P, NODES, PACK], BF16, name="x_copy")
-            nc.scalar.copy(out=x_copy[:].bitcast(F32), in_=xt[:].rearrange("p u n -> p n u"))
-            pair = pair_pool.tile([P, NODES, PACK], F32, name="pair")
+            totals[k] = ax
+
+        def transpose(k):
+            x_sb, _ = loaded[k]
+            x_words = x_sb[:].bitcast(F32)
+            x_copy = copy_pool.tile([P, IMAGES, NODES, PACK], BF16, name="x_copy")
+            values[k] = []
+            for j in range(len(images_of(k))):
+                xt = work_pool.tile([P, 2, NODES], F32, name="xt")
+                for u in range(2):
+                    for h in range(HALVES):
+                        nc.tensor.transpose(
+                            out=xt[:, u, h * P : (h + 1) * P],
+                            in_=x_words[:, j * HALVES + h, u : K_PASS // 2 : 2],
+                            identity=ident_words[:],
+                        )
+                nc.scalar.copy(out=x_copy[:, j].bitcast(F32), in_=xt[:].rearrange("p u n -> p n u"))
+                values[k].append(xt[:].bitcast(BF16).rearrange("p u (n e) -> p n u e", e=2))
+            pair = pair_pool.tile([P, IMAGES, NODES, PACK], F32, name="pair")
             nc.scalar.copy(
-                out=pair[:].rearrange("p (r c) t -> p r (c t)", c=GRID_COLS)[:, 0 : GRID_ROWS : GRID_ROWS - 1, :],
-                in_=x_copy[:].rearrange("p (r c) t -> p r (c t)", c=GRID_COLS)[:, 1 : GRID_ROWS - 1 : GRID_ROWS - 3, :],
+                out=used(k, pair).rearrange("p j (r c) t -> p j r (c t)", c=GRID_COLS)[
+                    :, :, 0 : GRID_ROWS : GRID_ROWS - 1, :
+                ],
+                in_=used(k, x_copy).rearrange("p j (r c) t -> p j r (c t)", c=GRID_COLS)[
+                    :, :, 1 : GRID_ROWS - 1 : GRID_ROWS - 3, :
+                ],
             )
-            values[u] = xt[:].bitcast(BF16).rearrange("p u (n e) -> p n u e", e=2)
-            copies[u] = x_copy
-            pairs[u] = pair
+            copies[k] = x_copy
+            pairs[k] = pair
 
-        def add_rows(u):
-            nc.vector.tensor_tensor(
-                out=lanes(pairs[u][:, GRID_COLS : NODES - GRID_COLS, :]),
-                in0=values[u][:, 2 * GRID_COLS :, :, :],
-                in1=lanes(copies[u][:, 0 : NODES - 2 * GRID_COLS, :]),
-                op=ADD,
-            )
-
-        def add_own_row(u):
-            triple = triple_pool.tile([P, NODES, PACK], F32, name="triple")
-            nc.vector.tensor_tensor(out=lanes(triple[:]), in0=values[u], in1=lanes(pairs[u][:]), op=ADD)
-            triples[u] = triple
-
-        def add_columns(u):
-            side = sides_pool.tile([P, GRID_ROWS, GRID_COLS * PACK], F32, name="side")
-            triple = triples[u][:].rearrange("p (r c) t -> p r (c t)", c=GRID_COLS)
-            nc.gpsimd.tensor_tensor(
-                out=side[:, :, PACK : (GRID_COLS - 1) * PACK],
-                in0=triple[:, :, 0 : (GRID_COLS - 2) * PACK],
-                in1=triple[:, :, 2 * PACK :],
-                op=ADD,
-            )
-            nc.scalar.copy(
-                out=side[:].rearrange("p r (c t) -> p r c t", t=PACK)[:, :, 0 : GRID_COLS : GRID_COLS - 1, :],
-                in_=triple.rearrange("p r (c t) -> p r c t", t=PACK)[:, :, 1 : GRID_COLS - 1 : GRID_COLS - 3, :],
-            )
-            sides[u] = side
-
-        def add_up(u):
-            ax = ax_pool.tile([P, NODES, PACK], BF16, name="ax", align_bytes=64)
-            nc.vector.tensor_tensor(
-                out=ax[:].rearrange("p n t -> p (n t)"),
-                in0=sides[u][:].rearrange("p r w -> p (r w)"),
-                in1=pairs[u][:].rearrange("p n t -> p (n t)"),
-                op=ADD,
-            )
-            totals[u] = ax
-
-        def multiply(u):
-            g, i = u // IMAGES, u % IMAGES
-            codes = mx_pool.tile([P, NODES], U32, name="codes", align_bytes=64)
-            scales = mx_pool.tile([P, NODES], U8, name="scales", align_bytes=64)
-            nc.vector.quantize_mx(
-                out=codes[:].bitcast(FP8X4), scales=scales[:], in_=totals[u][:].rearrange("p n t -> p (n t)")
-            )
-            for h in range(HALVES):
-                cols = slice(h * P, (h + 1) * P)
-                nc.tensor.matmul_mx(
-                    out=acc[i * HALVES + h][:],
-                    lhsT=codes[:, cols].bitcast(FP8X4),
-                    lhsT_scale=scales[:, cols],
-                    rhs=weights[g][:].bitcast(FP8X4),
-                    rhs_scale=w_scales[:, g, :],
-                    start=(g == 0),
-                    stop=(g == GROUPS - 1),
+        def add_rows(k):
+            for j in range(len(images_of(k))):
+                nc.vector.tensor_tensor(
+                    out=lanes(pairs[k][:, j, GRID_COLS : NODES - GRID_COLS, :]),
+                    in0=values[k][j][:, 2 * GRID_COLS :, :, :],
+                    in1=lanes(copies[k][:, j, 0 : NODES - 2 * GRID_COLS, :]),
+                    op=ADD,
                 )
 
-        steps = len(VECTOR_UNITS)
+        def add_own_row(k):
+            triple = triple_pool.tile([P, IMAGES, NODES, PACK], F32, name="triple")
+            for j in range(len(images_of(k))):
+                nc.vector.tensor_tensor(
+                    out=lanes(triple[:, j]), in0=values[k][j], in1=lanes(pairs[k][:, j]), op=ADD
+                )
+            triples[k] = triple
+
+        def add_columns(k):
+            side = sides_pool.tile([P, IMAGES, NODES, PACK], F32, name="side")
+            side_rows = used(k, side).rearrange("p j (r c) t -> p (j r) (c t)", c=GRID_COLS)
+            triple_rows = used(k, triples[k]).rearrange("p j (r c) t -> p (j r) (c t)", c=GRID_COLS)
+            nc.gpsimd.tensor_tensor(
+                out=side_rows[:, :, PACK : (GRID_COLS - 1) * PACK],
+                in0=triple_rows[:, :, 0 : (GRID_COLS - 2) * PACK],
+                in1=triple_rows[:, :, 2 * PACK :],
+                op=ADD,
+            )
+            nc.scalar.copy(
+                out=side_rows.rearrange("p r (c t) -> p r c t", t=PACK)[:, :, 0 : GRID_COLS : GRID_COLS - 1, :],
+                in_=triple_rows.rearrange("p r (c t) -> p r c t", t=PACK)[
+                    :, :, 1 : GRID_COLS - 1 : GRID_COLS - 3, :
+                ],
+            )
+            sides[k] = side
+
+        def add_up(k):
+            ax = ax_pool.tile([P, IMAGES, NODES, PACK], BF16, name="ax", align_bytes=64)
+            nc.vector.tensor_tensor(
+                out=used(k, ax).rearrange("p j n t -> p (j n t)"),
+                in0=used(k, sides[k]).rearrange("p j n t -> p (j n t)"),
+                in1=used(k, pairs[k]).rearrange("p j n t -> p (j n t)"),
+                op=ADD,
+            )
+            totals[k] = ax
+
+        passes_done = [0] * IMAGES
+
+        def multiply(k):
+            g, images = BATCHES[k]
+            nodes = len(images) * NODES
+            codes = mx_pool.tile([P, IMAGES * NODES], U32, name="codes", align_bytes=64)
+            scales = mx_pool.tile([P, IMAGES * NODES], U8, name="scales", align_bytes=64)
+            nc.vector.quantize_mx(
+                out=codes[:, 0:nodes].bitcast(FP8X4),
+                scales=scales[:, 0:nodes],
+                in_=used(k, totals[k]).rearrange("p j n t -> p (j n t)"),
+            )
+            for j, i in enumerate(images):
+                for h in range(HALVES):
+                    cols = slice((j * HALVES + h) * P, (j * HALVES + h + 1) * P)
+                    nc.tensor.matmul_mx(
+                        out=acc[i * HALVES + h][:],
+                        lhsT=codes[:, cols].bitcast(FP8X4),
+                        lhsT_scale=scales[:, cols],
+                        rhs=weights[g][:].bitcast(FP8X4),
+                        rhs_scale=w_scales[:, g, :],
+                        start=(passes_done[i] == 0),
+                        stop=(passes_done[i] == GROUPS - 1),
+                    )
+                passes_done[i] += 1
+
+        steps = len(VECTOR_BATCHES)
         loads_written = 0
-        prepared = 0
-        multiplied = 0
+        summed = []
         with tc.manual_schedule():
-            for step in range(steps + 4):
-                upto = VECTOR_UNITS[step + 1] + 1 if step + 1 < steps else UNITS
-                for u in range(loads_written, min(upto + LOADS_AHEAD, UNITS)):
-                    load(u)
-                    if u == 1:
+            for step in range(-1, steps + 3):
+                upto = VECTOR_BATCHES[step + 1] if step + 1 < steps else len(BATCHES)
+                for k in range(loads_written, min(upto + 1 + LOADS_AHEAD, len(BATCHES))):
+                    load(k)
+                    if k == 1:
                         for quadrant in range(4):
                             nc.sync.dma_start(
                                 out=w_scales[32 * quadrant : 32 * quadrant + 4, :, :].bitcast(I32),
                                 in_=s_view[4 * quadrant : 4 * quadrant + 4, :, :].bitcast(I32),
                             )
-                loads_written = max(loads_written, min(upto + LOADS_AHEAD, UNITS))
-                for u in sorted(range(prepared, upto), key=lambda u: u not in VECTOR_UNITS):
-                    prepare(u)
-                prepared = upto
+                loads_written = max(loads_written, min(upto + 1 + LOADS_AHEAD, len(BATCHES)))
 
-                if 0 <= step - 4 < steps:
-                    for u in range(multiplied, VECTOR_UNITS[step - 4] + 1):
-                        multiply(u)
-                    multiplied = VECTOR_UNITS[step - 4] + 1
-                if 0 <= step - 3 < steps:
-                    add_up(VECTOR_UNITS[step - 3])
-                if step < steps:
-                    add_rows(VECTOR_UNITS[step])
-                if 0 <= step - 1 < steps:
-                    add_own_row(VECTOR_UNITS[step - 1])
+                ready = list(summed)
+                summed.clear()
+                if 0 <= step < steps:
+                    for k in range(VECTOR_BATCHES[step] + 1, upto):
+                        sums_on_tensor(k)
+                        summed.append(k)
+
+                for k in ready:
+                    multiply(k)
                 if 0 <= step - 2 < steps:
-                    add_columns(VECTOR_UNITS[step - 2])
+                    add_up(VECTOR_BATCHES[step - 2])
+                if 0 <= step - 3 < steps:
+                    multiply(VECTOR_BATCHES[step - 3])
+                if 0 <= step < steps:
+                    add_rows(VECTOR_BATCHES[step])
+                    add_own_row(VECTOR_BATCHES[step])
+                if 0 <= step - 1 < steps:
+                    add_columns(VECTOR_BATCHES[step - 1])
+
+                if step + 1 < steps:
+                    transpose(VECTOR_BATCHES[step + 1])
 
         for m in range(IMAGES * HALVES):
             result = res_pool.tile([P, OUT_FEATURES], F32, name="result")

@@ -28,17 +28,24 @@ OFFSETS = [(-1, 0), (1, 0), (0, -1), (0, 1), (-1, -1), (-1, 1), (1, -1), (1, 1)]
 FLOPS = 2 * IMAGES * NODES * FEATURES * OUT_FEATURES
 
 TENSOR_PERIOD = 5
-TENSOR_TURNS = (2, 4)
-BATCHES = [(0, (0,)), (0, (1,))] + [(g, tuple(range(IMAGES))) for g in range(1, GROUPS)]
+TENSOR_TURNS = (1, 3)
+BATCHES = [(g, tuple(range(IMAGES))) for g in range(GROUPS - 1)] + [(GROUPS - 1, (1,)), (GROUPS - 1, (0,))]
 
 
 def on_tensor(batch):
-    return batch == (0, (1,)) or batch[0] % TENSOR_PERIOD in TENSOR_TURNS
+    if batch[0] == GROUPS - 1:
+        return batch[1] == (1,)
+    return batch[0] % TENSOR_PERIOD in TENSOR_TURNS
 
 
 VECTOR_BATCHES = [k for k, batch in enumerate(BATCHES) if not on_tensor(batch)]
 TENSOR_UNITS = sum(len(batch[1]) for batch in BATCHES if on_tensor(batch))
 assert 10 * TENSOR_UNITS * 2 * P * P * NODES * PACK <= FLOPS
+
+def rows_on_gpsimd(k):
+    rows = len(BATCHES[k][1]) * GRID_ROWS
+    return rows - GRID_ROWS if k in VECTOR_BATCHES[-2:] else rows
+
 
 LOADS_AHEAD = 3
 
@@ -58,17 +65,16 @@ def tile_graphconvlayer_k_kernel(tc, X, Wm_words, Wm_scales, b, H, W, out):
         x_pool = ctx.enter_context(tc.tile_pool(name="x", bufs=LOADS_AHEAD + 4))
         w_pool = ctx.enter_context(tc.tile_pool(name="w", bufs=LOADS_AHEAD + 9))
         copy_pool = ctx.enter_context(tc.tile_pool(name="copies", bufs=2))
-        pair_pool = ctx.enter_context(tc.tile_pool(name="pairs", bufs=4))
+        pair_pool = ctx.enter_context(tc.tile_pool(name="pairs", bufs=5))
         triple_pool = ctx.enter_context(tc.tile_pool(name="triples", bufs=2))
-        sides_pool = ctx.enter_context(tc.tile_pool(name="sides", bufs=1))
+        sides_pool = ctx.enter_context(tc.tile_pool(name="sides", bufs=2))
         ax_pool = ctx.enter_context(tc.tile_pool(name="ax", bufs=6))
         mx_pool = ctx.enter_context(tc.tile_pool(name="mx", bufs=3))
-        res_pool = ctx.enter_context(tc.tile_pool(name="res", bufs=2))
+        res_pool = ctx.enter_context(tc.tile_pool(name="res", bufs=IMAGES * HALVES))
         acc_pool = ctx.enter_context(tc.psum_pool(name="acc", bufs=1))
         work_pool = ctx.enter_context(tc.psum_pool(name="work", bufs=2))
 
         w_scales = const.tile([P, GROUPS, OUT_FEATURES], U8, align_bytes=64)
-        nc.vector.memset(w_scales[:].rearrange("p g n -> p (g n)").bitcast(I32), 0)
 
         bias = const.tile([P, OUT_FEATURES], BF16)
         nc.scalar.dma_start(out=bias[:], in_=b.partition_broadcast(P))
@@ -94,6 +100,7 @@ def tile_graphconvlayer_k_kernel(tc, X, Wm_words, Wm_scales, b, H, W, out):
                 op=ADD,
             )
         adjacency = adjacency_grid[:].rearrange("p r c -> p (r c)")
+        nc.gpsimd.memset(w_scales[:].rearrange("p g n -> p (g n)").bitcast(I32), 0)
 
         acc = [acc_pool.tile([P, OUT_FEATURES], F32, name="acc%d" % m) for m in range(IMAGES * HALVES)]
 
@@ -118,9 +125,14 @@ def tile_graphconvlayer_k_kernel(tc, X, Wm_words, Wm_scales, b, H, W, out):
         def load(k):
             g, images = BATCHES[k]
             features = slice(g * K_PASS, (g + 1) * K_PASS)
-            blocks = slice(images[0] * HALVES, (images[-1] + 1) * HALVES)
             x_sb = x_pool.tile([P, IMAGES * HALVES, K_PASS], BF16, name="x_sb")
-            nc.sync.dma_start(out=x_sb[:, 0 : len(images) * HALVES, :], in_=x_view[:, blocks, features])
+            if k == 0:
+                for i in images:
+                    blocks = slice(i * HALVES, (i + 1) * HALVES)
+                    nc.sync.dma_start(out=x_sb[:, blocks, :], in_=x_view[:, blocks, features])
+            else:
+                blocks = slice(images[0] * HALVES, (images[-1] + 1) * HALVES)
+                nc.sync.dma_start(out=x_sb[:, 0 : len(images) * HALVES, :], in_=x_view[:, blocks, features])
             if g not in weights:
                 w_sb = w_pool.tile([P, OUT_FEATURES], U32, name="w_sb", align_bytes=64)
                 nc.sync.dma_start(out=w_sb[:].bitcast(I32), in_=w_view[g].bitcast(I32))
@@ -167,6 +179,7 @@ def tile_graphconvlayer_k_kernel(tc, X, Wm_words, Wm_scales, b, H, W, out):
             x_sb, _ = loaded[k]
             x_words = x_sb[:].bitcast(F32)
             x_copy = copy_pool.tile([P, IMAGES, NODES, PACK], BF16, name="x_copy")
+            pair = pair_pool.tile([P, IMAGES, NODES, PACK], F32, name="pair")
             values[k] = []
             for j in range(len(images_of(k))):
                 xt = work_pool.tile([P, 2, NODES], F32, name="xt")
@@ -178,16 +191,15 @@ def tile_graphconvlayer_k_kernel(tc, X, Wm_words, Wm_scales, b, H, W, out):
                             identity=ident_words[:],
                         )
                 nc.scalar.copy(out=x_copy[:, j].bitcast(F32), in_=xt[:].rearrange("p u n -> p n u"))
+                nc.scalar.copy(
+                    out=pair[:, j].rearrange("p (r c) t -> p r (c t)", c=GRID_COLS)[
+                        :, 0 : GRID_ROWS : GRID_ROWS - 1, :
+                    ],
+                    in_=x_copy[:, j].rearrange("p (r c) t -> p r (c t)", c=GRID_COLS)[
+                        :, 1 : GRID_ROWS - 1 : GRID_ROWS - 3, :
+                    ],
+                )
                 values[k].append(xt[:].bitcast(BF16).rearrange("p u (n e) -> p n u e", e=2))
-            pair = pair_pool.tile([P, IMAGES, NODES, PACK], F32, name="pair")
-            nc.scalar.copy(
-                out=used(k, pair).rearrange("p j (r c) t -> p j r (c t)", c=GRID_COLS)[
-                    :, :, 0 : GRID_ROWS : GRID_ROWS - 1, :
-                ],
-                in_=used(k, x_copy).rearrange("p j (r c) t -> p j r (c t)", c=GRID_COLS)[
-                    :, :, 1 : GRID_ROWS - 1 : GRID_ROWS - 3, :
-                ],
-            )
             copies[k] = x_copy
             pairs[k] = pair
 
@@ -212,12 +224,18 @@ def tile_graphconvlayer_k_kernel(tc, X, Wm_words, Wm_scales, b, H, W, out):
             side = sides_pool.tile([P, IMAGES, NODES, PACK], F32, name="side")
             side_rows = used(k, side).rearrange("p j (r c) t -> p (j r) (c t)", c=GRID_COLS)
             triple_rows = used(k, triples[k]).rearrange("p j (r c) t -> p (j r) (c t)", c=GRID_COLS)
-            nc.gpsimd.tensor_tensor(
-                out=side_rows[:, :, PACK : (GRID_COLS - 1) * PACK],
-                in0=triple_rows[:, :, 0 : (GRID_COLS - 2) * PACK],
-                in1=triple_rows[:, :, 2 * PACK :],
-                op=ADD,
-            )
+            cut = rows_on_gpsimd(k)
+            for engine, rows in (
+                (nc.gpsimd, slice(0, cut)),
+                (nc.vector, slice(cut, len(images_of(k)) * GRID_ROWS)),
+            ):
+                if rows.start < rows.stop:
+                    engine.tensor_tensor(
+                        out=side_rows[:, rows, PACK : (GRID_COLS - 1) * PACK],
+                        in0=triple_rows[:, rows, 0 : (GRID_COLS - 2) * PACK],
+                        in1=triple_rows[:, rows, 2 * PACK :],
+                        op=ADD,
+                    )
             nc.scalar.copy(
                 out=side_rows.rearrange("p r (c t) -> p r c t", t=PACK)[:, :, 0 : GRID_COLS : GRID_COLS - 1, :],
                 in_=triple_rows.rearrange("p r (c t) -> p r c t", t=PACK)[
@@ -266,11 +284,11 @@ def tile_graphconvlayer_k_kernel(tc, X, Wm_words, Wm_scales, b, H, W, out):
         loads_written = 0
         summed = []
         with tc.manual_schedule():
-            for step in range(-1, steps + 3):
+            for step in range(-1, steps + 4):
                 upto = VECTOR_BATCHES[step + 1] if step + 1 < steps else len(BATCHES)
                 for k in range(loads_written, min(upto + 1 + LOADS_AHEAD, len(BATCHES))):
                     load(k)
-                    if k == 1:
+                    if k == 2:
                         for quadrant in range(4):
                             nc.sync.dma_start(
                                 out=w_scales[32 * quadrant : 32 * quadrant + 4, :, :].bitcast(I32),
@@ -287,20 +305,20 @@ def tile_graphconvlayer_k_kernel(tc, X, Wm_words, Wm_scales, b, H, W, out):
 
                 for k in ready:
                     multiply(k)
-                if 0 <= step - 2 < steps:
-                    add_up(VECTOR_BATCHES[step - 2])
                 if 0 <= step - 3 < steps:
-                    multiply(VECTOR_BATCHES[step - 3])
+                    add_up(VECTOR_BATCHES[step - 3])
+                if 0 <= step - 4 < steps:
+                    multiply(VECTOR_BATCHES[step - 4])
+                if 0 <= step - 1 < steps:
+                    add_columns(VECTOR_BATCHES[step - 1])
                 if 0 <= step < steps:
                     add_rows(VECTOR_BATCHES[step])
                     add_own_row(VECTOR_BATCHES[step])
-                if 0 <= step - 1 < steps:
-                    add_columns(VECTOR_BATCHES[step - 1])
 
                 if step + 1 < steps:
                     transpose(VECTOR_BATCHES[step + 1])
 
-        for m in range(IMAGES * HALVES):
+        for m in reversed(range(IMAGES * HALVES)):
             result = res_pool.tile([P, OUT_FEATURES], F32, name="result")
             nc.vector.tensor_tensor(out=result[:], in0=acc[m][:], in1=bias[:], op=ADD)
             nc.sync.dma_start(out=out_view[m], in_=result[:])

@@ -39,8 +39,8 @@ def on_tensor(batch):
 
 
 VECTOR_BATCHES = [k for k, batch in enumerate(BATCHES) if not on_tensor(batch)]
-TENSOR_UNITS = sum(len(batch[1]) for batch in BATCHES if on_tensor(batch))
-assert 10 * TENSOR_UNITS * 2 * P * P * NODES * PACK <= FLOPS
+TENSOR_UNITS = [(k, j) for k, batch in enumerate(BATCHES) if on_tensor(batch) for j in range(len(batch[1]))]
+assert 10 * len(TENSOR_UNITS) * 2 * P * P * NODES * PACK <= FLOPS
 
 def rows_on_gpsimd(k):
     rows = len(BATCHES[k][1]) * GRID_ROWS
@@ -62,7 +62,7 @@ def tile_graphconvlayer_k_kernel(tc, X, Wm_words, Wm_scales, b, H, W, out):
 
     with ExitStack() as ctx:
         const = ctx.enter_context(tc.tile_pool(name="const", bufs=1))
-        x_pool = ctx.enter_context(tc.tile_pool(name="x", bufs=LOADS_AHEAD + 4))
+        x_pool = ctx.enter_context(tc.tile_pool(name="x", bufs=LOADS_AHEAD + 5))
         w_pool = ctx.enter_context(tc.tile_pool(name="w", bufs=LOADS_AHEAD + 9))
         copy_pool = ctx.enter_context(tc.tile_pool(name="copies", bufs=2))
         pair_pool = ctx.enter_context(tc.tile_pool(name="pairs", bufs=5))
@@ -143,37 +143,30 @@ def tile_graphconvlayer_k_kernel(tc, X, Wm_words, Wm_scales, b, H, W, out):
                 nc.sync.dma_start(out=used(k, x_mid), in_=x_mid_view[:, images[0] : images[-1] + 1, features])
             loaded[k] = (x_sb, x_mid)
 
-        def sums_on_tensor(k):
+        def sums_on_tensor(k, j):
             x_sb, x_mid = loaded[k]
             row = GRID_COLS
-            ax = ax_pool.tile([P, IMAGES, NODES, PACK], BF16, name="ax", align_bytes=64)
-            for j in range(len(images_of(k))):
-                for h in range(HALVES):
-                    sums = work_pool.tile([P, PACK, P], F32, name="sums")
-                    for t in range(PACK):
-                        k_cols = slice(t, K_PASS, PACK)
-                        if h == 0:
-                            parts = (
-                                (slice(0, P - row), x_sb[:, j * HALVES, k_cols], slice(0, P - row)),
-                                (slice(P - row, P), x_mid[:, j, k_cols], slice(P // 2 - row, P // 2)),
-                            )
-                        else:
-                            parts = (
-                                (slice(0, row), x_mid[:, j, k_cols], slice(P // 2, P // 2 + row)),
-                                (slice(row, P), x_sb[:, j * HALVES + 1, k_cols], slice(row, P)),
-                            )
-                        for nodes, values_in, neighbours in parts:
-                            nc.tensor.matmul(
-                                out=sums[:, t, nodes],
-                                lhsT=values_in,
-                                rhs=adjacency[:, neighbours],
-                                start=True,
-                                stop=True,
-                            )
-                    nc.scalar.copy(
-                        out=ax[:, j, h * P : (h + 1) * P, :], in_=sums[:].rearrange("p t n -> p n t")
-                    )
-            totals[k] = ax
+            if j == 0:
+                totals[k] = ax_pool.tile([P, IMAGES, NODES, PACK], BF16, name="ax", align_bytes=64)
+            for u in range(2):
+                sums = work_pool.tile([P, 2, NODES], F32, name="sums")
+                for e in range(2):
+                    k_cols = slice(2 * u + e, K_PASS, PACK)
+                    for nodes, values_in, neighbours in (
+                        (slice(0, P - row), x_sb[:, j * HALVES, k_cols], slice(0, P - row)),
+                        (slice(P - row, P + row), x_mid[:, j, k_cols], slice(P // 2 - row, P // 2 + row)),
+                        (slice(P + row, NODES), x_sb[:, j * HALVES + 1, k_cols], slice(row, P)),
+                    ):
+                        nc.tensor.matmul(
+                            out=sums[:, e, nodes],
+                            lhsT=values_in,
+                            rhs=adjacency[:, neighbours],
+                            start=True,
+                            stop=True,
+                        )
+                nc.scalar.copy(
+                    out=totals[k][:, j, :, 2 * u : 2 * u + 2], in_=sums[:].rearrange("p e n -> p n e")
+                )
 
         def transpose(k):
             x_sb, _ = loaded[k]
@@ -282,7 +275,8 @@ def tile_graphconvlayer_k_kernel(tc, X, Wm_words, Wm_scales, b, H, W, out):
 
         steps = len(VECTOR_BATCHES)
         loads_written = 0
-        summed = []
+        summed = 0
+        ready = []
         with tc.manual_schedule():
             for step in range(-1, steps + 4):
                 upto = VECTOR_BATCHES[step + 1] if step + 1 < steps else len(BATCHES)
@@ -296,14 +290,16 @@ def tile_graphconvlayer_k_kernel(tc, X, Wm_words, Wm_scales, b, H, W, out):
                             )
                 loads_written = max(loads_written, min(upto + 1 + LOADS_AHEAD, len(BATCHES)))
 
-                ready = list(summed)
-                summed.clear()
-                if 0 <= step < steps:
-                    for k in range(VECTOR_BATCHES[step] + 1, upto):
-                        sums_on_tensor(k)
-                        summed.append(k)
+                to_quantise = list(ready)
+                ready.clear()
+                share = min(len(TENSOR_UNITS) * (step + 1) // steps, len(TENSOR_UNITS))
+                for k, j in TENSOR_UNITS[summed:share]:
+                    sums_on_tensor(k, j)
+                    if j + 1 == len(images_of(k)):
+                        ready.append(k)
+                summed = share
 
-                for k in ready:
+                for k in to_quantise:
                     multiply(k)
                 if 0 <= step - 3 < steps:
                     add_up(VECTOR_BATCHES[step - 3])

@@ -27,20 +27,29 @@ OFFSETS = [(-1, 0), (1, 0), (0, -1), (0, 1), (-1, -1), (-1, 1), (1, -1), (1, 1)]
 
 FLOPS = 2 * IMAGES * NODES * FEATURES * OUT_FEATURES
 
+PAIR = 2
 TENSOR_PERIOD = 5
 TENSOR_TURNS = (1, 3)
-BATCHES = [(g, tuple(range(IMAGES))) for g in range(GROUPS - 1)] + [(GROUPS - 1, (1,)), (GROUPS - 1, (0,))]
+LAST_PAIR = GROUPS // PAIR - 1
 
 
-def on_tensor(batch):
-    if batch[0] == GROUPS - 1:
-        return batch[1] == (1,)
-    return batch[0] % TENSOR_PERIOD in TENSOR_TURNS
+def make_batches():
+    batches = []
+    for i in range(IMAGES):
+        for n in range(GROUPS // PAIR):
+            groups = tuple(range(n * PAIR, (n + 1) * PAIR))
+            if i == IMAGES - 1 and n == LAST_PAIR:
+                batches.extend([(i, groups[:1], True), (i, groups[1:], False)])
+            else:
+                batches.append((i, groups, n % TENSOR_PERIOD in TENSOR_TURNS))
+    return batches
 
 
-VECTOR_BATCHES = [k for k, batch in enumerate(BATCHES) if not on_tensor(batch)]
-TENSOR_UNITS = [(k, j) for k, batch in enumerate(BATCHES) if on_tensor(batch) for j in range(len(batch[1]))]
+BATCHES = make_batches()
+VECTOR_BATCHES = [k for k, batch in enumerate(BATCHES) if not batch[2]]
+TENSOR_UNITS = [(k, j) for k, batch in enumerate(BATCHES) if batch[2] for j in range(len(batch[1]))]
 assert 10 * len(TENSOR_UNITS) * 2 * P * P * NODES * PACK <= FLOPS
+
 
 def rows_on_gpsimd(k):
     rows = len(BATCHES[k][1]) * GRID_ROWS
@@ -48,32 +57,34 @@ def rows_on_gpsimd(k):
 
 
 LOADS_AHEAD = 3
+WEIGHTS_BEHIND = 4
 
 
 def tile_graphconvlayer_k_kernel(tc, X, Wm_words, Wm_scales, b, H, W, out):
     nc = tc.nc
     assert H == GRID_ROWS and W == GRID_COLS
 
-    x_view = X.rearrange("i (h p) k -> p (i h) k", p=P)
-    x_mid_view = X[:, P // 2 : P // 2 + P, :].rearrange("i p k -> p i k")
-    w_view = Wm_words.rearrange("g p n t -> g p (n t)")
+    x_view = X.rearrange("i (h p) k -> i p h k", p=P)
+    w_view = Wm_words.rearrange("g p n t -> p g (n t)")
     s_view = Wm_scales.rearrange("g q n -> q g n")
-    out_view = out.rearrange("i (h p) n -> (i h) p n", p=P)
+    out_view = out.rearrange("i (h p) n -> i h p n", p=P)
 
     with ExitStack() as ctx:
         const = ctx.enter_context(tc.tile_pool(name="const", bufs=1))
         x_pool = ctx.enter_context(tc.tile_pool(name="x", bufs=LOADS_AHEAD + 5))
-        w_pool = ctx.enter_context(tc.tile_pool(name="w", bufs=LOADS_AHEAD + 9))
+        mid_pool = ctx.enter_context(tc.tile_pool(name="mid", bufs=4))
         copy_pool = ctx.enter_context(tc.tile_pool(name="copies", bufs=2))
-        pair_pool = ctx.enter_context(tc.tile_pool(name="pairs", bufs=5))
+        pair_pool = ctx.enter_context(tc.tile_pool(name="pairs", bufs=4))
         triple_pool = ctx.enter_context(tc.tile_pool(name="triples", bufs=2))
         sides_pool = ctx.enter_context(tc.tile_pool(name="sides", bufs=2))
-        ax_pool = ctx.enter_context(tc.tile_pool(name="ax", bufs=6))
+        ax_pool = ctx.enter_context(tc.tile_pool(name="ax", bufs=3))
         mx_pool = ctx.enter_context(tc.tile_pool(name="mx", bufs=3))
-        res_pool = ctx.enter_context(tc.tile_pool(name="res", bufs=IMAGES * HALVES))
+        res_pool = ctx.enter_context(tc.tile_pool(name="res", bufs=HALVES))
         acc_pool = ctx.enter_context(tc.psum_pool(name="acc", bufs=1))
-        work_pool = ctx.enter_context(tc.psum_pool(name="work", bufs=2))
+        xt_pool = ctx.enter_context(tc.psum_pool(name="xt", bufs=2 * PAIR))
+        sums_pool = ctx.enter_context(tc.psum_pool(name="sums", bufs=2))
 
+        w_words = const.tile([P, GROUPS, OUT_FEATURES], U32, align_bytes=64)
         w_scales = const.tile([P, GROUPS, OUT_FEATURES], U8, align_bytes=64)
 
         bias = const.tile([P, OUT_FEATURES], BF16)
@@ -102,10 +113,7 @@ def tile_graphconvlayer_k_kernel(tc, X, Wm_words, Wm_scales, b, H, W, out):
         adjacency = adjacency_grid[:].rearrange("p r c -> p (r c)")
         nc.gpsimd.memset(w_scales[:].rearrange("p g n -> p (g n)").bitcast(I32), 0)
 
-        acc = [acc_pool.tile([P, OUT_FEATURES], F32, name="acc%d" % m) for m in range(IMAGES * HALVES)]
-
         loaded = {}
-        weights = {}
         values = {}
         copies = {}
         pairs = {}
@@ -116,46 +124,57 @@ def tile_graphconvlayer_k_kernel(tc, X, Wm_words, Wm_scales, b, H, W, out):
         def lanes(ap):
             return ap.rearrange("p n (u e) -> p n u e", e=2)
 
-        def images_of(k):
+        def lanes_in_psum(xt):
+            return xt[:].bitcast(BF16).rearrange("p u (n e) -> p n u e", e=2)
+
+        def groups_of(k):
             return BATCHES[k][1]
 
         def used(k, tile):
-            return tile[:, 0 : len(images_of(k))]
+            return tile[:, 0 : len(groups_of(k))]
 
         def load(k):
-            g, images = BATCHES[k]
-            features = slice(g * K_PASS, (g + 1) * K_PASS)
-            x_sb = x_pool.tile([P, IMAGES * HALVES, K_PASS], BF16, name="x_sb")
-            if k == 0:
-                for i in images:
-                    blocks = slice(i * HALVES, (i + 1) * HALVES)
-                    nc.sync.dma_start(out=x_sb[:, blocks, :], in_=x_view[:, blocks, features])
-            else:
-                blocks = slice(images[0] * HALVES, (images[-1] + 1) * HALVES)
-                nc.sync.dma_start(out=x_sb[:, 0 : len(images) * HALVES, :], in_=x_view[:, blocks, features])
-            if g not in weights:
-                w_sb = w_pool.tile([P, OUT_FEATURES], U32, name="w_sb", align_bytes=64)
-                nc.sync.dma_start(out=w_sb[:].bitcast(I32), in_=w_view[g].bitcast(I32))
-                weights[g] = w_sb
+            i, groups, on_tensor = BATCHES[k]
+            x_sb = x_pool.tile([P, HALVES, PAIR * K_PASS], BF16, name="x_sb")
+            pieces = [(g,) for g in groups] if k == 0 else [groups]
+            for piece in pieces:
+                first = (piece[0] - groups[0]) * K_PASS
+                width = len(piece) * K_PASS
+                nc.sync.dma_start(
+                    out=x_sb[:, :, first : first + width],
+                    in_=x_view[i, :, :, piece[0] * K_PASS : piece[0] * K_PASS + width],
+                )
             x_mid = None
-            if k not in VECTOR_BATCHES:
-                x_mid = x_pool.tile([P, IMAGES, K_PASS], BF16, name="x_mid")
-                nc.sync.dma_start(out=used(k, x_mid), in_=x_mid_view[:, images[0] : images[-1] + 1, features])
+            if on_tensor:
+                width = len(groups) * K_PASS
+                x_mid = mid_pool.tile([P, PAIR * K_PASS], BF16, name="x_mid")
+                nc.sync.dma_start(
+                    out=x_mid[:, 0:width],
+                    in_=X[i, P // 2 : P // 2 + P, groups[0] * K_PASS : groups[0] * K_PASS + width],
+                )
             loaded[k] = (x_sb, x_mid)
+
+        def load_weights(k):
+            i, groups, _ = BATCHES[k]
+            if i == 0:
+                members = slice(groups[0], groups[-1] + 1)
+                nc.sync.dma_start(
+                    out=w_words[:, members, :].bitcast(I32), in_=w_view[:, members, :].bitcast(I32)
+                )
 
         def sums_on_tensor(k, j):
             x_sb, x_mid = loaded[k]
             row = GRID_COLS
             if j == 0:
-                totals[k] = ax_pool.tile([P, IMAGES, NODES, PACK], BF16, name="ax", align_bytes=64)
+                totals[k] = ax_pool.tile([P, PAIR, NODES, PACK], BF16, name="ax_tensor", align_bytes=64)
             for u in range(2):
-                sums = work_pool.tile([P, 2, NODES], F32, name="sums")
+                sums = sums_pool.tile([P, 2, NODES], F32, name="sums")
                 for e in range(2):
-                    k_cols = slice(2 * u + e, K_PASS, PACK)
+                    k_cols = slice(j * K_PASS + 2 * u + e, (j + 1) * K_PASS, PACK)
                     for nodes, values_in, neighbours in (
-                        (slice(0, P - row), x_sb[:, j * HALVES, k_cols], slice(0, P - row)),
-                        (slice(P - row, P + row), x_mid[:, j, k_cols], slice(P // 2 - row, P // 2 + row)),
-                        (slice(P + row, NODES), x_sb[:, j * HALVES + 1, k_cols], slice(row, P)),
+                        (slice(0, P - row), x_sb[:, 0, k_cols], slice(0, P - row)),
+                        (slice(P - row, P + row), x_mid[:, k_cols], slice(P // 2 - row, P // 2 + row)),
+                        (slice(P + row, NODES), x_sb[:, 1, k_cols], slice(row, P)),
                     ):
                         nc.tensor.matmul(
                             out=sums[:, e, nodes],
@@ -171,18 +190,22 @@ def tile_graphconvlayer_k_kernel(tc, X, Wm_words, Wm_scales, b, H, W, out):
         def transpose(k):
             x_sb, _ = loaded[k]
             x_words = x_sb[:].bitcast(F32)
-            x_copy = copy_pool.tile([P, IMAGES, NODES, PACK], BF16, name="x_copy")
-            pair = pair_pool.tile([P, IMAGES, NODES, PACK], F32, name="pair")
             values[k] = []
-            for j in range(len(images_of(k))):
-                xt = work_pool.tile([P, 2, NODES], F32, name="xt")
+            for j in range(len(groups_of(k))):
+                xt = xt_pool.tile([P, 2, NODES], F32, name="xt")
                 for u in range(2):
                     for h in range(HALVES):
                         nc.tensor.transpose(
                             out=xt[:, u, h * P : (h + 1) * P],
-                            in_=x_words[:, j * HALVES + h, u : K_PASS // 2 : 2],
+                            in_=x_words[:, h, j * K_PASS // 2 + u : (j + 1) * K_PASS // 2 : 2],
                             identity=ident_words[:],
                         )
+                values[k].append(xt)
+
+        def copy_out(k):
+            x_copy = copy_pool.tile([P, PAIR, NODES, PACK], BF16, name="x_copy")
+            pair = pair_pool.tile([P, PAIR, NODES, PACK], F32, name="pair")
+            for j, xt in enumerate(values[k]):
                 nc.scalar.copy(out=x_copy[:, j].bitcast(F32), in_=xt[:].rearrange("p u n -> p n u"))
                 nc.scalar.copy(
                     out=pair[:, j].rearrange("p (r c) t -> p r (c t)", c=GRID_COLS)[
@@ -192,35 +215,34 @@ def tile_graphconvlayer_k_kernel(tc, X, Wm_words, Wm_scales, b, H, W, out):
                         :, 1 : GRID_ROWS - 1 : GRID_ROWS - 3, :
                     ],
                 )
-                values[k].append(xt[:].bitcast(BF16).rearrange("p u (n e) -> p n u e", e=2))
             copies[k] = x_copy
             pairs[k] = pair
 
         def add_rows(k):
-            for j in range(len(images_of(k))):
+            for j, xt in enumerate(values[k]):
                 nc.vector.tensor_tensor(
                     out=lanes(pairs[k][:, j, GRID_COLS : NODES - GRID_COLS, :]),
-                    in0=values[k][j][:, 2 * GRID_COLS :, :, :],
+                    in0=lanes_in_psum(xt)[:, 2 * GRID_COLS :, :, :],
                     in1=lanes(copies[k][:, j, 0 : NODES - 2 * GRID_COLS, :]),
                     op=ADD,
                 )
 
         def add_own_row(k):
-            triple = triple_pool.tile([P, IMAGES, NODES, PACK], F32, name="triple")
-            for j in range(len(images_of(k))):
+            triple = triple_pool.tile([P, PAIR, NODES, PACK], F32, name="triple")
+            for j, xt in enumerate(values[k]):
                 nc.vector.tensor_tensor(
-                    out=lanes(triple[:, j]), in0=values[k][j], in1=lanes(pairs[k][:, j]), op=ADD
+                    out=lanes(triple[:, j]), in0=lanes_in_psum(xt), in1=lanes(pairs[k][:, j]), op=ADD
                 )
             triples[k] = triple
 
         def add_columns(k):
-            side = sides_pool.tile([P, IMAGES, NODES, PACK], F32, name="side")
+            side = sides_pool.tile([P, PAIR, NODES, PACK], F32, name="side")
             side_rows = used(k, side).rearrange("p j (r c) t -> p (j r) (c t)", c=GRID_COLS)
             triple_rows = used(k, triples[k]).rearrange("p j (r c) t -> p (j r) (c t)", c=GRID_COLS)
             cut = rows_on_gpsimd(k)
             for engine, rows in (
                 (nc.gpsimd, slice(0, cut)),
-                (nc.vector, slice(cut, len(images_of(k)) * GRID_ROWS)),
+                (nc.vector, slice(cut, len(groups_of(k)) * GRID_ROWS)),
             ):
                 if rows.start < rows.stop:
                     engine.tensor_tensor(
@@ -238,7 +260,7 @@ def tile_graphconvlayer_k_kernel(tc, X, Wm_words, Wm_scales, b, H, W, out):
             sides[k] = side
 
         def add_up(k):
-            ax = ax_pool.tile([P, IMAGES, NODES, PACK], BF16, name="ax", align_bytes=64)
+            ax = ax_pool.tile([P, PAIR, NODES, PACK], BF16, name="ax", align_bytes=64)
             nc.vector.tensor_tensor(
                 out=used(k, ax).rearrange("p j n t -> p (j n t)"),
                 in0=used(k, sides[k]).rearrange("p j n t -> p (j n t)"),
@@ -247,42 +269,52 @@ def tile_graphconvlayer_k_kernel(tc, X, Wm_words, Wm_scales, b, H, W, out):
             )
             totals[k] = ax
 
-        passes_done = [0] * IMAGES
+        acc = {}
 
         def multiply(k):
-            g, images = BATCHES[k]
-            nodes = len(images) * NODES
-            codes = mx_pool.tile([P, IMAGES * NODES], U32, name="codes", align_bytes=64)
-            scales = mx_pool.tile([P, IMAGES * NODES], U8, name="scales", align_bytes=64)
+            i, groups, _ = BATCHES[k]
+            nodes = len(groups) * NODES
+            codes = mx_pool.tile([P, PAIR * NODES], U32, name="codes", align_bytes=64)
+            scales = mx_pool.tile([P, PAIR * NODES], U8, name="scales", align_bytes=64)
             nc.vector.quantize_mx(
                 out=codes[:, 0:nodes].bitcast(FP8X4),
                 scales=scales[:, 0:nodes],
                 in_=used(k, totals[k]).rearrange("p j n t -> p (j n t)"),
             )
-            for j, i in enumerate(images):
+            for j, g in enumerate(groups):
                 for h in range(HALVES):
+                    if g == 0:
+                        acc[i, h] = acc_pool.tile([P, OUT_FEATURES], F32, name="acc%d" % h)
                     cols = slice((j * HALVES + h) * P, (j * HALVES + h + 1) * P)
                     nc.tensor.matmul_mx(
-                        out=acc[i * HALVES + h][:],
+                        out=acc[i, h][:],
                         lhsT=codes[:, cols].bitcast(FP8X4),
                         lhsT_scale=scales[:, cols],
-                        rhs=weights[g][:].bitcast(FP8X4),
+                        rhs=w_words[:, g, :].bitcast(FP8X4),
                         rhs_scale=w_scales[:, g, :],
-                        start=(passes_done[i] == 0),
-                        stop=(passes_done[i] == GROUPS - 1),
+                        start=(g == 0),
+                        stop=(g == GROUPS - 1),
                     )
-                passes_done[i] += 1
+
+        def finish(i):
+            for h in range(HALVES):
+                result = res_pool.tile([P, OUT_FEATURES], F32, name="result")
+                nc.vector.tensor_tensor(out=result[:], in0=acc[i, h][:], in1=bias[:], op=ADD)
+                nc.sync.dma_start(out=out_view[i, h], in_=result[:])
 
         steps = len(VECTOR_BATCHES)
         loads_written = 0
         summed = 0
-        ready = []
+        multiplied = 0
+        finished = 0
         with tc.manual_schedule():
             for step in range(-1, steps + 4):
                 upto = VECTOR_BATCHES[step + 1] if step + 1 < steps else len(BATCHES)
                 for k in range(loads_written, min(upto + 1 + LOADS_AHEAD, len(BATCHES))):
                     load(k)
-                    if k == 2:
+                    if k >= WEIGHTS_BEHIND:
+                        load_weights(k - WEIGHTS_BEHIND)
+                    if k == WEIGHTS_BEHIND + 2:
                         for quadrant in range(4):
                             nc.sync.dma_start(
                                 out=w_scales[32 * quadrant : 32 * quadrant + 4, :, :].bitcast(I32),
@@ -290,31 +322,29 @@ def tile_graphconvlayer_k_kernel(tc, X, Wm_words, Wm_scales, b, H, W, out):
                             )
                 loads_written = max(loads_written, min(upto + 1 + LOADS_AHEAD, len(BATCHES)))
 
-                to_quantise = list(ready)
-                ready.clear()
-                share = min(len(TENSOR_UNITS) * (step + 1) // steps, len(TENSOR_UNITS))
+                if step + 1 < steps:
+                    transpose(VECTOR_BATCHES[step + 1])
+                share = max(0, min(len(TENSOR_UNITS) * step // steps, len(TENSOR_UNITS)))
                 for k, j in TENSOR_UNITS[summed:share]:
                     sums_on_tensor(k, j)
-                    if j + 1 == len(images_of(k)):
-                        ready.append(k)
                 summed = share
 
-                for k in to_quantise:
-                    multiply(k)
+                if 0 <= step - 4 < steps:
+                    for k in range(multiplied, VECTOR_BATCHES[step - 4]):
+                        multiply(k)
                 if 0 <= step - 3 < steps:
                     add_up(VECTOR_BATCHES[step - 3])
                 if 0 <= step - 4 < steps:
                     multiply(VECTOR_BATCHES[step - 4])
+                    multiplied = VECTOR_BATCHES[step - 4] + 1
                 if 0 <= step - 1 < steps:
                     add_columns(VECTOR_BATCHES[step - 1])
+                if step + 1 < steps:
+                    copy_out(VECTOR_BATCHES[step + 1])
                 if 0 <= step < steps:
                     add_rows(VECTOR_BATCHES[step])
                     add_own_row(VECTOR_BATCHES[step])
 
-                if step + 1 < steps:
-                    transpose(VECTOR_BATCHES[step + 1])
-
-        for m in reversed(range(IMAGES * HALVES)):
-            result = res_pool.tile([P, OUT_FEATURES], F32, name="result")
-            nc.vector.tensor_tensor(out=result[:], in0=acc[m][:], in1=bias[:], op=ADD)
-            nc.sync.dma_start(out=out_view[m], in_=result[:])
+                while finished < IMAGES and all(k < multiplied for k, batch in enumerate(BATCHES) if batch[0] == finished):
+                    finish(finished)
+                    finished += 1

@@ -48,16 +48,22 @@ def make_batches():
 BATCHES = make_batches()
 VECTOR_BATCHES = [k for k, batch in enumerate(BATCHES) if not batch[2]]
 TENSOR_UNITS = [(k, j) for k, batch in enumerate(BATCHES) if batch[2] for j in range(len(batch[1]))]
-assert 10 * len(TENSOR_UNITS) * 2 * P * P * NODES * PACK <= FLOPS
+SHARED = VECTOR_BATCHES[-1]
+assert 10 * (len(TENSOR_UNITS) * NODES + P) * PACK * 2 * P * P <= FLOPS
+
+
+def first_row(k):
+    return BLOCK_ROWS if k == SHARED else 0
 
 
 def rows_on_gpsimd(k):
-    rows = len(BATCHES[k][1]) * GRID_ROWS
-    return rows - GRID_ROWS if k in VECTOR_BATCHES[-2:] else rows
+    later = [n for n in VECTOR_BATCHES if n > k]
+    return len(BATCHES[later[0]][1]) * GRID_ROWS - first_row(later[0]) if later else 0
 
 
 LOADS_AHEAD = 3
 WEIGHTS_BEHIND = 4
+BIAS_BEHIND = GROUPS // PAIR // 2
 
 
 def tile_graphconvlayer_k_kernel(tc, X, Wm_words, Wm_scales, b, H, W, out):
@@ -88,7 +94,6 @@ def tile_graphconvlayer_k_kernel(tc, X, Wm_words, Wm_scales, b, H, W, out):
         w_scales = const.tile([P, GROUPS, OUT_FEATURES], U8, align_bytes=64)
 
         bias = const.tile([P, OUT_FEATURES], BF16)
-        nc.scalar.dma_start(out=bias[:], in_=b.partition_broadcast(P))
 
         ident_words = const.tile([P, P], F32)
         make_identity(nc, ident_words[:])
@@ -145,7 +150,7 @@ def tile_graphconvlayer_k_kernel(tc, X, Wm_words, Wm_scales, b, H, W, out):
                     in_=x_view[i, :, :, piece[0] * K_PASS : piece[0] * K_PASS + width],
                 )
             x_mid = None
-            if on_tensor:
+            if on_tensor or k == SHARED:
                 width = len(groups) * K_PASS
                 x_mid = mid_pool.tile([P, PAIR * K_PASS], BF16, name="x_mid")
                 nc.sync.dma_start(
@@ -187,6 +192,26 @@ def tile_graphconvlayer_k_kernel(tc, X, Wm_words, Wm_scales, b, H, W, out):
                     out=totals[k][:, j, :, 2 * u : 2 * u + 2], in_=sums[:].rearrange("p e n -> p n e")
                 )
 
+        def upper_sums_on_tensor(k):
+            x_sb, x_mid = loaded[k]
+            row = GRID_COLS
+            totals[k] = ax_pool.tile([P, PAIR, NODES, PACK], BF16, name="ax", align_bytes=64)
+            sums = sums_pool.tile([P, PACK, P], F32, name="sums")
+            for t in range(PACK):
+                k_cols = slice(t, K_PASS, PACK)
+                for nodes, values_in, neighbours in (
+                    (slice(0, P - row), x_sb[:, 0, k_cols], slice(0, P - row)),
+                    (slice(P - row, P), x_mid[:, k_cols], slice(P // 2 - row, P // 2)),
+                ):
+                    nc.tensor.matmul(
+                        out=sums[:, t, nodes],
+                        lhsT=values_in,
+                        rhs=adjacency[:, neighbours],
+                        start=True,
+                        stop=True,
+                    )
+            nc.scalar.copy(out=totals[k][:, 0, 0:P, :], in_=sums[:].rearrange("p t n -> p n t"))
+
         def transpose(k):
             x_sb, _ = loaded[k]
             x_words = x_sb[:].bitcast(F32)
@@ -207,31 +232,37 @@ def tile_graphconvlayer_k_kernel(tc, X, Wm_words, Wm_scales, b, H, W, out):
             pair = pair_pool.tile([P, PAIR, NODES, PACK], F32, name="pair")
             for j, xt in enumerate(values[k]):
                 nc.scalar.copy(out=x_copy[:, j].bitcast(F32), in_=xt[:].rearrange("p u n -> p n u"))
-                nc.scalar.copy(
-                    out=pair[:, j].rearrange("p (r c) t -> p r (c t)", c=GRID_COLS)[
-                        :, 0 : GRID_ROWS : GRID_ROWS - 1, :
-                    ],
-                    in_=x_copy[:, j].rearrange("p (r c) t -> p r (c t)", c=GRID_COLS)[
-                        :, 1 : GRID_ROWS - 1 : GRID_ROWS - 3, :
-                    ],
-                )
+                pair_rows = pair[:, j].rearrange("p (r c) t -> p r (c t)", c=GRID_COLS)
+                copy_rows = x_copy[:, j].rearrange("p (r c) t -> p r (c t)", c=GRID_COLS)
+                if first_row(k) == 0:
+                    nc.scalar.copy(
+                        out=pair_rows[:, 0 : GRID_ROWS : GRID_ROWS - 1, :],
+                        in_=copy_rows[:, 1 : GRID_ROWS - 1 : GRID_ROWS - 3, :],
+                    )
+                else:
+                    nc.scalar.copy(out=pair_rows[:, GRID_ROWS - 1, :], in_=copy_rows[:, GRID_ROWS - 2, :])
             copies[k] = x_copy
             pairs[k] = pair
 
         def add_rows(k):
+            first = max(first_row(k), 1) * GRID_COLS
             for j, xt in enumerate(values[k]):
                 nc.vector.tensor_tensor(
-                    out=lanes(pairs[k][:, j, GRID_COLS : NODES - GRID_COLS, :]),
-                    in0=lanes_in_psum(xt)[:, 2 * GRID_COLS :, :, :],
-                    in1=lanes(copies[k][:, j, 0 : NODES - 2 * GRID_COLS, :]),
+                    out=lanes(pairs[k][:, j, first : NODES - GRID_COLS, :]),
+                    in0=lanes_in_psum(xt)[:, first + GRID_COLS :, :, :],
+                    in1=lanes(copies[k][:, j, first - GRID_COLS : NODES - 2 * GRID_COLS, :]),
                     op=ADD,
                 )
 
         def add_own_row(k):
+            first = first_row(k) * GRID_COLS
             triple = triple_pool.tile([P, PAIR, NODES, PACK], F32, name="triple")
             for j, xt in enumerate(values[k]):
                 nc.vector.tensor_tensor(
-                    out=lanes(triple[:, j]), in0=lanes_in_psum(xt), in1=lanes(pairs[k][:, j]), op=ADD
+                    out=lanes(triple[:, j, first:]),
+                    in0=lanes_in_psum(xt)[:, first:, :, :],
+                    in1=lanes(pairs[k][:, j, first:]),
+                    op=ADD,
                 )
             triples[k] = triple
 
@@ -239,11 +270,10 @@ def tile_graphconvlayer_k_kernel(tc, X, Wm_words, Wm_scales, b, H, W, out):
             side = sides_pool.tile([P, PAIR, NODES, PACK], F32, name="side")
             side_rows = used(k, side).rearrange("p j (r c) t -> p (j r) (c t)", c=GRID_COLS)
             triple_rows = used(k, triples[k]).rearrange("p j (r c) t -> p (j r) (c t)", c=GRID_COLS)
-            cut = rows_on_gpsimd(k)
-            for engine, rows in (
-                (nc.gpsimd, slice(0, cut)),
-                (nc.vector, slice(cut, len(groups_of(k)) * GRID_ROWS)),
-            ):
+            first = first_row(k)
+            last = len(groups_of(k)) * GRID_ROWS
+            cut = max(first, min(last, rows_on_gpsimd(k)))
+            for engine, rows in ((nc.gpsimd, slice(first, cut)), (nc.vector, slice(cut, last))):
                 if rows.start < rows.stop:
                     engine.tensor_tensor(
                         out=side_rows[:, rows, PACK : (GRID_COLS - 1) * PACK],
@@ -252,22 +282,25 @@ def tile_graphconvlayer_k_kernel(tc, X, Wm_words, Wm_scales, b, H, W, out):
                         op=ADD,
                     )
             nc.scalar.copy(
-                out=side_rows.rearrange("p r (c t) -> p r c t", t=PACK)[:, :, 0 : GRID_COLS : GRID_COLS - 1, :],
+                out=side_rows.rearrange("p r (c t) -> p r c t", t=PACK)[
+                    :, first:, 0 : GRID_COLS : GRID_COLS - 1, :
+                ],
                 in_=triple_rows.rearrange("p r (c t) -> p r c t", t=PACK)[
-                    :, :, 1 : GRID_COLS - 1 : GRID_COLS - 3, :
+                    :, first:, 1 : GRID_COLS - 1 : GRID_COLS - 3, :
                 ],
             )
             sides[k] = side
 
         def add_up(k):
-            ax = ax_pool.tile([P, PAIR, NODES, PACK], BF16, name="ax", align_bytes=64)
+            if k != SHARED:
+                totals[k] = ax_pool.tile([P, PAIR, NODES, PACK], BF16, name="ax", align_bytes=64)
+            first = first_row(k) * GRID_COLS
             nc.vector.tensor_tensor(
-                out=used(k, ax).rearrange("p j n t -> p (j n t)"),
-                in0=used(k, sides[k]).rearrange("p j n t -> p (j n t)"),
-                in1=used(k, pairs[k]).rearrange("p j n t -> p (j n t)"),
+                out=used(k, totals[k])[:, :, first:, :],
+                in0=used(k, sides[k])[:, :, first:, :],
+                in1=used(k, pairs[k])[:, :, first:, :],
                 op=ADD,
             )
-            totals[k] = ax
 
         acc = {}
 
@@ -314,6 +347,8 @@ def tile_graphconvlayer_k_kernel(tc, X, Wm_words, Wm_scales, b, H, W, out):
                     load(k)
                     if k >= WEIGHTS_BEHIND:
                         load_weights(k - WEIGHTS_BEHIND)
+                    if k == BIAS_BEHIND:
+                        nc.sync.dma_start(out=bias[:], in_=b.partition_broadcast(P))
                     if k == WEIGHTS_BEHIND + 2:
                         for quadrant in range(4):
                             nc.sync.dma_start(
@@ -328,6 +363,8 @@ def tile_graphconvlayer_k_kernel(tc, X, Wm_words, Wm_scales, b, H, W, out):
                 for k, j in TENSOR_UNITS[summed:share]:
                     sums_on_tensor(k, j)
                 summed = share
+                if step == steps:
+                    upper_sums_on_tensor(SHARED)
 
                 if 0 <= step - 4 < steps:
                     for k in range(multiplied, VECTOR_BATCHES[step - 4]):

@@ -52,6 +52,12 @@ SHARED = VECTOR_BATCHES[-1]
 assert 10 * (len(TENSOR_UNITS) * NODES + P) * PACK * 2 * P * P <= FLOPS
 
 
+def with_vector_batch(v):
+    if not 0 <= v < len(VECTOR_BATCHES):
+        return []
+    return list(range(VECTOR_BATCHES[v - 1] + 1 if v > 0 else 0, VECTOR_BATCHES[v] + 1))
+
+
 def first_row(k):
     return BLOCK_ROWS if k == SHARED else 0
 
@@ -62,8 +68,10 @@ def rows_on_gpsimd(k):
 
 
 LOADS_AHEAD = 3
-WEIGHTS_BEHIND = 4
-BIAS_BEHIND = GROUPS // PAIR // 2
+TENSOR_BEHIND = 1
+WEIGHTS_BEHIND = 2
+SCALES_AT = 3
+BIAS_AT = 6
 
 
 def tile_graphconvlayer_k_kernel(tc, X, Wm_words, Wm_scales, b, H, W, out):
@@ -77,7 +85,7 @@ def tile_graphconvlayer_k_kernel(tc, X, Wm_words, Wm_scales, b, H, W, out):
 
     with ExitStack() as ctx:
         const = ctx.enter_context(tc.tile_pool(name="const", bufs=1))
-        x_pool = ctx.enter_context(tc.tile_pool(name="x", bufs=LOADS_AHEAD + 5))
+        x_pool = ctx.enter_context(tc.tile_pool(name="x", bufs=LOADS_AHEAD + 6))
         mid_pool = ctx.enter_context(tc.tile_pool(name="mid", bufs=4))
         copy_pool = ctx.enter_context(tc.tile_pool(name="copies", bufs=2))
         pair_pool = ctx.enter_context(tc.tile_pool(name="pairs", bufs=4))
@@ -342,24 +350,29 @@ def tile_graphconvlayer_k_kernel(tc, X, Wm_words, Wm_scales, b, H, W, out):
         finished = 0
         with tc.manual_schedule():
             for step in range(-1, steps + 4):
-                upto = VECTOR_BATCHES[step + 1] if step + 1 < steps else len(BATCHES)
-                for k in range(loads_written, min(upto + 1 + LOADS_AHEAD, len(BATCHES))):
-                    load(k)
-                    if k >= WEIGHTS_BEHIND:
-                        load_weights(k - WEIGHTS_BEHIND)
-                    if k == BIAS_BEHIND:
-                        nc.sync.dma_start(out=bias[:], in_=b.partition_broadcast(P))
-                    if k == WEIGHTS_BEHIND + 2:
+                upto = min(step + 2 + LOADS_AHEAD, steps + WEIGHTS_BEHIND)
+                for v in range(loads_written, upto):
+                    for k in with_vector_batch(v):
+                        if k in VECTOR_BATCHES:
+                            load(k)
+                    if v == SCALES_AT:
                         for quadrant in range(4):
                             nc.sync.dma_start(
                                 out=w_scales[32 * quadrant : 32 * quadrant + 4, :, :].bitcast(I32),
                                 in_=s_view[4 * quadrant : 4 * quadrant + 4, :, :].bitcast(I32),
                             )
-                loads_written = max(loads_written, min(upto + 1 + LOADS_AHEAD, len(BATCHES)))
+                    for k in with_vector_batch(v - TENSOR_BEHIND):
+                        if k not in VECTOR_BATCHES:
+                            load(k)
+                    for k in with_vector_batch(v - WEIGHTS_BEHIND):
+                        load_weights(k)
+                    if v == BIAS_AT:
+                        nc.sync.dma_start(out=bias[:], in_=b.partition_broadcast(P))
+                loads_written = max(loads_written, upto)
 
                 if step + 1 < steps:
                     transpose(VECTOR_BATCHES[step + 1])
-                share = max(0, min(len(TENSOR_UNITS) * step // steps, len(TENSOR_UNITS)))
+                share = min(len(TENSOR_UNITS) * step // steps, len(TENSOR_UNITS)) if step >= 2 else 0
                 for k, j in TENSOR_UNITS[summed:share]:
                     sums_on_tensor(k, j)
                 summed = share
@@ -369,11 +382,13 @@ def tile_graphconvlayer_k_kernel(tc, X, Wm_words, Wm_scales, b, H, W, out):
                 if 0 <= step - 4 < steps:
                     for k in range(multiplied, VECTOR_BATCHES[step - 4]):
                         multiply(k)
-                if 0 <= step - 3 < steps:
+                if 0 <= step - 3 < steps - 1:
                     add_up(VECTOR_BATCHES[step - 3])
                 if 0 <= step - 4 < steps:
                     multiply(VECTOR_BATCHES[step - 4])
                     multiplied = VECTOR_BATCHES[step - 4] + 1
+                if step - 3 == steps - 1:
+                    add_up(VECTOR_BATCHES[step - 3])
                 if 0 <= step - 1 < steps:
                     add_columns(VECTOR_BATCHES[step - 1])
                 if step + 1 < steps:

from contextlib import ExitStack

import concourse.mybir as mybir
from concourse.masks import make_identity

F32 = mybir.dt.float32
BF16 = mybir.dt.bfloat16
I32 = mybir.dt.int32
U32 = mybir.dt.uint32
U8 = mybir.dt.uint8
FP8X4 = mybir.dt.float8_e4m3fn_x4
ADD = mybir.AluOpType.add

P = 128
PACK = 4
K_PASS = P * PACK
IMAGES = 2
GRID_ROWS = 16
GRID_COLS = 16
NODES = GRID_ROWS * GRID_COLS
HALVES = NODES // P
BLOCK_ROWS = P // GRID_COLS
FEATURES = 16384
OUT_FEATURES = 512
GROUPS = FEATURES // K_PASS
OFFSETS = [(-1, 0), (1, 0), (0, -1), (0, 1), (-1, -1), (-1, 1), (1, -1), (1, 1)]

FLOPS = 2 * IMAGES * NODES * FEATURES * OUT_FEATURES

PAIR = 2
TENSOR_PERIOD = 5
TENSOR_TURNS = (1, 3)
LAST_PAIR = GROUPS // PAIR - 1


def make_batches():
    batches = []
    for i in range(IMAGES):
        for n in range(GROUPS // PAIR):
            groups = tuple(range(n * PAIR, (n + 1) * PAIR))
            if i == IMAGES - 1 and n == LAST_PAIR:
                batches.extend([(i, groups[:1], True), (i, groups[1:], False)])
            else:
                batches.append((i, groups, n % TENSOR_PERIOD in TENSOR_TURNS))
    return batches


BATCHES = make_batches()
VECTOR_BATCHES = [k for k, batch in enumerate(BATCHES) if not batch[2]]
TENSOR_UNITS = [(k, j) for k, batch in enumerate(BATCHES) if batch[2] for j in range(len(batch[1]))]
SHARED = VECTOR_BATCHES[-1]
assert 10 * (len(TENSOR_UNITS) * NODES + P) * PACK * 2 * P * P <= FLOPS


def with_vector_batch(v):
    if not 0 <= v < len(VECTOR_BATCHES):
        return []
    return list(range(VECTOR_BATCHES[v - 1] + 1 if v > 0 else 0, VECTOR_BATCHES[v] + 1))


def first_row(k):
    return BLOCK_ROWS if k == SHARED else 0


def rows_on_gpsimd(k):
    later = [n for n in VECTOR_BATCHES if n > k]
    return len(BATCHES[later[0]][1]) * GRID_ROWS - first_row(later[0]) if later else 0


LOADS_AHEAD = 3
TENSOR_BEHIND = 1
WEIGHTS_BEHIND = 2
SCALES_AT = 3
BIAS_AT = 6


def tile_graphconvlayer_k_kernel(tc, X, Wm_words, Wm_scales, b, H, W, out):
    nc = tc.nc
    assert H == GRID_ROWS and W == GRID_COLS

    x_view = X.rearrange("i (h p) k -> i p h k", p=P)
    w_view = Wm_words.rearrange("g p n t -> p g (n t)")
    s_view = Wm_scales.rearrange("g q n -> q g n")
    out_view = out.rearrange("i (h p) n -> i h p n", p=P)

    with ExitStack() as ctx:
        const = ctx.enter_context(tc.tile_pool(name="const", bufs=1))
        x_pool = ctx.enter_context(tc.tile_pool(name="x", bufs=LOADS_AHEAD + 6))
        mid_pool = ctx.enter_context(tc.tile_pool(name="mid", bufs=4))
        copy_pool = ctx.enter_context(tc.tile_pool(name="copies", bufs=2))
        pair_pool = ctx.enter_context(tc.tile_pool(name="pairs", bufs=4))
        triple_pool = ctx.enter_context(tc.tile_pool(name="triples", bufs=2))
        sides_pool = ctx.enter_context(tc.tile_pool(name="sides", bufs=2))
        ax_pool = ctx.enter_context(tc.tile_pool(name="ax", bufs=3))
        mx_pool = ctx.enter_context(tc.tile_pool(name="mx", bufs=3))
        res_pool = ctx.enter_context(tc.tile_pool(name="res", bufs=HALVES))
        acc_pool = ctx.enter_context(tc.psum_pool(name="acc", bufs=1))
        xt_pool = ctx.enter_context(tc.psum_pool(name="xt", bufs=2 * PAIR))
        sums_pool = ctx.enter_context(tc.psum_pool(name="sums", bufs=2))

        w_words = const.tile([P, GROUPS, OUT_FEATURES], U32, align_bytes=64)
        w_scales = const.tile([P, GROUPS, OUT_FEATURES], U8, align_bytes=64)

        bias = const.tile([P, OUT_FEATURES], BF16)

        ident_words = const.tile([P, P], F32)
        make_identity(nc, ident_words[:])

        ident = const.tile([P, P], BF16)
        make_identity(nc, ident[:])
        unit_grid = const.tile([P, BLOCK_ROWS + 2, GRID_COLS + 2], BF16)
        nc.gpsimd.memset(unit_grid[:], 0.0)
        nc.vector.tensor_copy(
            out=unit_grid[:, 1 : 1 + BLOCK_ROWS, 1 : 1 + GRID_COLS],
            in_=ident[:].rearrange("p (r c) -> p r c", c=GRID_COLS),
        )
        adjacency_grid = const.tile([P, BLOCK_ROWS, GRID_COLS], BF16)
        nc.gpsimd.memset(adjacency_grid[:], 0.0)
        for dr, dc in OFFSETS:
            nc.vector.tensor_tensor(
                out=adjacency_grid[:],
                in0=adjacency_grid[:],
                in1=unit_grid[:, 1 + dr : 1 + dr + BLOCK_ROWS, 1 + dc : 1 + dc + GRID_COLS],
                op=ADD,
            )
        adjacency = adjacency_grid[:].rearrange("p r c -> p (r c)")
        nc.gpsimd.memset(w_scales[:].rearrange("p g n -> p (g n)").bitcast(I32), 0)

        loaded = {}
        values = {}
        copies = {}
        pairs = {}
        triples = {}
        sides = {}
        totals = {}

        def lanes(ap):
            return ap.rearrange("p n (u e) -> p n u e", e=2)

        def lanes_in_psum(xt):
            return xt[:].bitcast(BF16).rearrange("p u (n e) -> p n u e", e=2)

        def groups_of(k):
            return BATCHES[k][1]

        def used(k, tile):
            return tile[:, 0 : len(groups_of(k))]

        def load(k):
            i, groups, on_tensor = BATCHES[k]
            x_sb = x_pool.tile([P, HALVES, PAIR * K_PASS], BF16, name="x_sb")
            pieces = [(g,) for g in groups] if k == 0 else [groups]
            for piece in pieces:
                first = (piece[0] - groups[0]) * K_PASS
                width = len(piece) * K_PASS
                nc.sync.dma_start(
                    out=x_sb[:, :, first : first + width],
                    in_=x_view[i, :, :, piece[0] * K_PASS : piece[0] * K_PASS + width],
                )
            x_mid = None
            if on_tensor or k == SHARED:
                width = len(groups) * K_PASS
                x_mid = mid_pool.tile([P, PAIR * K_PASS], BF16, name="x_mid")
                nc.sync.dma_start(
                    out=x_mid[:, 0:width],
                    in_=X[i, P // 2 : P // 2 + P, groups[0] * K_PASS : groups[0] * K_PASS + width],
                )
            loaded[k] = (x_sb, x_mid)

        def load_weights(k):
            i, groups, _ = BATCHES[k]
            if i == 0:
                members = slice(groups[0], groups[-1] + 1)
                nc.sync.dma_start(
                    out=w_words[:, members, :].bitcast(I32), in_=w_view[:, members, :].bitcast(I32)
                )

        def sums_on_tensor(k, j):
            x_sb, x_mid = loaded[k]
            row = GRID_COLS
            if j == 0:
                totals[k] = ax_pool.tile([P, PAIR, NODES, PACK], BF16, name="ax_tensor", align_bytes=64)
            for u in range(2):
                sums = sums_pool.tile([P, 2, NODES], F32, name="sums")
                for e in range(2):
                    k_cols = slice(j * K_PASS + 2 * u + e, (j + 1) * K_PASS, PACK)
                    for nodes, values_in, neighbours in (
                        (slice(0, P - row), x_sb[:, 0, k_cols], slice(0, P - row)),
                        (slice(P - row, P + row), x_mid[:, k_cols], slice(P // 2 - row, P // 2 + row)),
                        (slice(P + row, NODES), x_sb[:, 1, k_cols], slice(row, P)),
                    ):
                        nc.tensor.matmul(
                            out=sums[:, e, nodes],
                            lhsT=values_in,
                            rhs=adjacency[:, neighbours],
                            start=True,
                            stop=True,
                        )
                nc.scalar.copy(
                    out=totals[k][:, j, :, 2 * u : 2 * u + 2], in_=sums[:].rearrange("p e n -> p n e")
                )

        def upper_sums_on_tensor(k):
            x_sb, x_mid = loaded[k]
            row = GRID_COLS
            totals[k] = ax_pool.tile([P, PAIR, NODES, PACK], BF16, name="ax", align_bytes=64)
            sums = sums_pool.tile([P, PACK, P], F32, name="sums")
            for t in range(PACK):
                k_cols = slice(t, K_PASS, PACK)
                for nodes, values_in, neighbours in (
                    (slice(0, P - row), x_sb[:, 0, k_cols], slice(0, P - row)),
                    (slice(P - row, P), x_mid[:, k_cols], slice(P // 2 - row, P // 2)),
                ):
                    nc.tensor.matmul(
                        out=sums[:, t, nodes],
                        lhsT=values_in,
                        rhs=adjacency[:, neighbours],
                        start=True,
                        stop=True,
                    )
            nc.scalar.copy(out=totals[k][:, 0, 0:P, :], in_=sums[:].rearrange("p t n -> p n t"))

        def transpose(k):
            x_sb, _ = loaded[k]
            x_words = x_sb[:].bitcast(F32)
            values[k] = []
            for j in range(len(groups_of(k))):
                xt = xt_pool.tile([P, 2, NODES], F32, name="xt")
                for u in range(2):
                    for h in range(HALVES):
                        nc.tensor.transpose(
                            out=xt[:, u, h * P : (h + 1) * P],
                            in_=x_words[:, h, j * K_PASS // 2 + u : (j + 1) * K_PASS // 2 : 2],
                            identity=ident_words[:],
                        )
                values[k].append(xt)

        def copy_out(k):
            x_copy = copy_pool.tile([P, PAIR, NODES, PACK], BF16, name="x_copy")
            pair = pair_pool.tile([P, PAIR, NODES, PACK], F32, name="pair")
            for j, xt in enumerate(values[k]):
                nc.scalar.copy(out=x_copy[:, j].bitcast(F32), in_=xt[:].rearrange("p u n -> p n u"))
                pair_rows = pair[:, j].rearrange("p (r c) t -> p r (c t)", c=GRID_COLS)
                copy_rows = x_copy[:, j].rearrange("p (r c) t -> p r (c t)", c=GRID_COLS)
                if first_row(k) == 0:
                    nc.scalar.copy(
                        out=pair_rows[:, 0 : GRID_ROWS : GRID_ROWS - 1, :],
                        in_=copy_rows[:, 1 : GRID_ROWS - 1 : GRID_ROWS - 3, :],
                    )
                else:
                    nc.scalar.copy(out=pair_rows[:, GRID_ROWS - 1, :], in_=copy_rows[:, GRID_ROWS - 2, :])
            copies[k] = x_copy
            pairs[k] = pair

        def add_rows(k):
            first = max(first_row(k), 1) * GRID_COLS
            for j, xt in enumerate(values[k]):
                nc.vector.tensor_tensor(
                    out=lanes(pairs[k][:, j, first : NODES - GRID_COLS, :]),
                    in0=lanes_in_psum(xt)[:, first + GRID_COLS :, :, :],
                    in1=lanes(copies[k][:, j, first - GRID_COLS : NODES - 2 * GRID_COLS, :]),
                    op=ADD,
                )

        def add_own_row(k):
            first = first_row(k) * GRID_COLS
            triple = triple_pool.tile([P, PAIR, NODES, PACK], F32, name="triple")
            for j, xt in enumerate(values[k]):
                nc.vector.tensor_tensor(
                    out=lanes(triple[:, j, first:]),
                    in0=lanes_in_psum(xt)[:, first:, :, :],
                    in1=lanes(pairs[k][:, j, first:]),
                    op=ADD,
                )
            triples[k] = triple

        def add_columns(k):
            side = sides_pool.tile([P, PAIR, NODES, PACK], F32, name="side")
            side_rows = used(k, side).rearrange("p j (r c) t -> p (j r) (c t)", c=GRID_COLS)
            triple_rows = used(k, triples[k]).rearrange("p j (r c) t -> p (j r) (c t)", c=GRID_COLS)
            first = first_row(k)
            last = len(groups_of(k)) * GRID_ROWS
            cut = max(first, min(last, rows_on_gpsimd(k)))
            for engine, rows in ((nc.gpsimd, slice(first, cut)), (nc.vector, slice(cut, last))):
                if rows.start < rows.stop:
                    engine.tensor_tensor(
                        out=side_rows[:, rows, PACK : (GRID_COLS - 1) * PACK],
                        in0=triple_rows[:, rows, 0 : (GRID_COLS - 2) * PACK],
                        in1=triple_rows[:, rows, 2 * PACK :],
                        op=ADD,
                    )
            nc.scalar.copy(
                out=side_rows.rearrange("p r (c t) -> p r c t", t=PACK)[
                    :, first:, 0 : GRID_COLS : GRID_COLS - 1, :
                ],
                in_=triple_rows.rearrange("p r (c t) -> p r c t", t=PACK)[
                    :, first:, 1 : GRID_COLS - 1 : GRID_COLS - 3, :
                ],
            )
            sides[k] = side

        def add_up(k):
            if k != SHARED:
                totals[k] = ax_pool.tile([P, PAIR, NODES, PACK], BF16, name="ax", align_bytes=64)
            first = first_row(k) * GRID_COLS
            nc.vector.tensor_tensor(
                out=used(k, totals[k])[:, :, first:, :],
                in0=used(k, sides[k])[:, :, first:, :],
                in1=used(k, pairs[k])[:, :, first:, :],
                op=ADD,
            )

        acc = {}

        def multiply(k):
            i, groups, _ = BATCHES[k]
            nodes = len(groups) * NODES
            codes = mx_pool.tile([P, PAIR * NODES], U32, name="codes", align_bytes=64)
            scales = mx_pool.tile([P, PAIR * NODES], U8, name="scales", align_bytes=64)
            nc.vector.quantize_mx(
                out=codes[:, 0:nodes].bitcast(FP8X4),
                scales=scales[:, 0:nodes],
                in_=used(k, totals[k]).rearrange("p j n t -> p (j n t)"),
            )
            for j, g in enumerate(groups):
                for h in range(HALVES):
                    if g == 0:
                        acc[i, h] = acc_pool.tile([P, OUT_FEATURES], F32, name="acc%d" % h)
                    cols = slice((j * HALVES + h) * P, (j * HALVES + h + 1) * P)
                    nc.tensor.matmul_mx(
                        out=acc[i, h][:],
                        lhsT=codes[:, cols].bitcast(FP8X4),
                        lhsT_scale=scales[:, cols],
                        rhs=w_words[:, g, :].bitcast(FP8X4),
                        rhs_scale=w_scales[:, g, :],
                        start=(g == 0),
                        stop=(g == GROUPS - 1),
                    )

        def finish(i):
            for h in range(HALVES):
                result = res_pool.tile([P, OUT_FEATURES], F32, name="result")
                nc.vector.tensor_tensor(out=result[:], in0=acc[i, h][:], in1=bias[:], op=ADD)
                nc.sync.dma_start(out=out_view[i, h], in_=result[:])

        steps = len(VECTOR_BATCHES)
        loads_written = 0
        summed = 0
        multiplied = 0
        finished = 0
        with tc.manual_schedule():
            for step in range(-1, steps + 4):
                upto = min(step + 2 + LOADS_AHEAD, steps + WEIGHTS_BEHIND)
                for v in range(loads_written, upto):
                    for k in with_vector_batch(v):
                        if k in VECTOR_BATCHES:
                            load(k)
                    if v == SCALES_AT:
                        for quadrant in range(4):
                            nc.sync.dma_start(
                                out=w_scales[32 * quadrant : 32 * quadrant + 4, :, :].bitcast(I32),
                                in_=s_view[4 * quadrant : 4 * quadrant + 4, :, :].bitcast(I32),
                            )
                    for k in with_vector_batch(v - TENSOR_BEHIND):
                        if k not in VECTOR_BATCHES:
                            load(k)
                    for k in with_vector_batch(v - WEIGHTS_BEHIND):
                        load_weights(k)
                    if v == BIAS_AT:
                        nc.sync.dma_start(out=bias[:], in_=b.partition_broadcast(P))
                loads_written = max(loads_written, upto)

                if step + 1 < steps:
                    transpose(VECTOR_BATCHES[step + 1])
                share = min(len(TENSOR_UNITS) * step // steps, len(TENSOR_UNITS)) if step >= 2 else 0
                for k, j in TENSOR_UNITS[summed:share]:
                    sums_on_tensor(k, j)
                summed = share
                if step == steps:
                    upper_sums_on_tensor(SHARED)

                if 0 <= step - 4 < steps:
                    for k in range(multiplied, VECTOR_BATCHES[step - 4]):
                        multiply(k)
                if 0 <= step - 3 < steps - 1:
                    add_up(VECTOR_BATCHES[step - 3])
                if 0 <= step - 4 < steps:
                    multiply(VECTOR_BATCHES[step - 4])
                    multiplied = VECTOR_BATCHES[step - 4] + 1
                if step - 3 == steps - 1:
                    add_up(VECTOR_BATCHES[step - 3])
                if 0 <= step - 1 < steps:
                    add_columns(VECTOR_BATCHES[step - 1])
                if step + 1 < steps:
                    copy_out(VECTOR_BATCHES[step + 1])
                if 0 <= step < steps:
                    add_rows(VECTOR_BATCHES[step])
                    add_own_row(VECTOR_BATCHES[step])

                while finished < IMAGES and all(k < multiplied for k, batch in enumerate(BATCHES) if batch[0] == finished):
                    finish(finished)
                    finished += 1
